import numpy as np
import ml_dtypes


def mxq(x, axis, fmt="e4m3"):
    dtype, down = {"e4m3": (ml_dtypes.float8_e4m3fn, 7), "e5m2": (ml_dtypes.float8_e5m2, 14)}[fmt]
    v = np.moveaxis(np.asarray(x, np.float32).astype(ml_dtypes.bfloat16).astype(np.float64), axis, -1)
    blocks = v.reshape(v.shape[:-1] + (-1, 32))
    amax = np.abs(blocks).max(-1, keepdims=True)
    byte = np.maximum(np.where(amax > 0, np.frexp(amax)[1] - 1 + 127, 0) - down, 1)
    scale = np.exp2(byte - 127.0)
    codes = (blocks / scale).astype(np.float32).astype(dtype).astype(np.float64)
    return np.moveaxis((codes * scale).reshape(v.shape), -1, axis)


WIDE = False


def mx_kscale(k):
    if not WIDE:
        return np.ones(k)
    levels = np.array([10, -10, 5, -5, 0])
    a = np.random.permutation(np.resize(levels, k // 512 * 4)).reshape(k // 512, 4)
    idx = np.arange(k)
    return np.exp2(a[idx // 512, idx % 128 // 32])


BF16 = ml_dtypes.bfloat16


def bf(x):
    return np.asarray(x, np.float32).astype(BF16)


def f64(x):
    return np.asarray(x).astype(np.float64)


B, C, T, H = 4, 512, 2048, 256
EPS_LN = 1e-5
EPS_STD = 1e-5


def ln_dim1(z, g, b):
    mu = z.mean(axis=1, keepdims=True)
    var = ((z - mu) ** 2).mean(axis=1, keepdims=True)
    return (z - mu) / np.sqrt(var + EPS_LN) * g[None, :, None] + b[None, :, None]


def stats(x, m):
    mean = (m * x).sum(axis=2)
    std = np.sqrt(np.maximum((m * x * x).sum(axis=2) - mean ** 2, EPS_STD))
    return mean, std


def setup_inputs():
    s = mx_kscale(C)
    lens = np.random.randint(T // 2, T, size=B)
    mask = (np.arange(T)[None, None, :] < lens[:, None, None]) * 1.0
    off = 0.5 * np.random.standard_normal((B, C, 1))
    gain = 0.5 + np.random.random((B, C, 1))
    pad = np.random.standard_normal((B, C, 1)) * (1.0 - mask)
    x = off + gain * np.random.standard_normal((B, C, T)) + pad
    return {"x": bf(x * s[None, :, None]),
            "mask": bf(mask),
            "w1": bf(np.random.standard_normal((H, 3 * C)) / np.sqrt(3 * C) / np.tile(s, 3)[None, :]),
            "b1": bf(0.1 * np.random.standard_normal(H)),
            "g1": bf(1.0 + 0.1 * np.random.standard_normal(H)),
            "be1": bf(0.1 * np.random.standard_normal(H))}


def reference(x, mask, w1, b1, g1, be1):
    x, mask = f64(x), f64(mask)
    total = mask.sum(axis=2, keepdims=True)
    mean0, std0 = stats(x, mask / total)
    mean0 = mean0
    std0 = std0
    x_in = np.concatenate([
        x,
        np.broadcast_to(mean0[:, :, None], (B, C, T)),
        np.broadcast_to(std0[:, :, None], (B, C, T)),
    ], axis=1)
    u = (mxq(f64(w1), 1, "e4m3") @ mxq(x_in, 1, "e4m3")) + f64(b1)[None, :, None]
    return np.tanh(ln_dim1(np.maximum(u, 0.0), f64(g1), f64(be1)))

@@ -1,0 +1,406 @@
+from contextlib import ExitStack
+
+import concourse.mybir as mybir
+from concourse.masks import make_identity
+
+F32 = mybir.dt.float32
+BF16 = mybir.dt.bfloat16
+U32 = mybir.dt.uint32
+U8 = mybir.dt.uint8
+FP8X4 = mybir.dt.float8_e4m3fn_x4
+ALU = mybir.AluOpType
+ACT = mybir.ActivationFunctionType
+AX = mybir.AxisListType
+
+B, C, T, H = 4, 512, 2048, 256
+P = 128
+PACK = 4
+CHUNK = 512
+NCH = T // CHUNK
+TILES = CHUNK // P
+NG = B * NCH
+NQ = T // P
+EPS_LN = 1e-5
+EPS_STD = 1e-5
+LEAD = 5
+P4O = 2
+RGA = 3
+P4V_FROM = 12
+BCS_AT = 1
+VSQ = [14,15]
+FLOPS = 2 * B * H * 3 * C * T
+
+
+def tile_attentivestatspool_pa_t_kernel(tc, x, mask, w1, b1, g1, be1, out):
+    nc = tc.nc
+    with ExitStack() as ctx:
+        const = ctx.enter_context(tc.tile_pool(name="const", bufs=1))
+        xmp = ctx.enter_context(tc.tile_pool(name="xmp", bufs=3))
+        grp = ctx.enter_context(tc.tile_pool(name="grp", bufs=6))
+        cod = ctx.enter_context(tc.tile_pool(name="cod", bufs=3))
+        sml = ctx.enter_context(tc.tile_pool(name="sml", bufs=6))
+        per = ctx.enter_context(tc.tile_pool(name="per", bufs=2))
+        up = ctx.enter_context(tc.tile_pool(name="up", bufs=5))
+        zp = ctx.enter_context(tc.tile_pool(name="zp", bufs=3))
+        op = ctx.enter_context(tc.tile_pool(name="op", bufs=3))
+        ps_mx = ctx.enter_context(tc.psum_pool(name="ps_mx", bufs=3))
+        ps_tr = ctx.enter_context(tc.psum_pool(name="ps_tr", bufs=3))
+        ps_ms = ctx.enter_context(tc.psum_pool(name="ps_ms", bufs=1))
+        ps_mk = ctx.enter_context(tc.psum_pool(name="ps_mk", bufs=1))
+        ctx.enter_context(tc.manual_schedule())
+
+        raw = [const.tile([P, PACK, T], BF16, name="raw%d" % b) for b in range(B)]
+        w1_sb = const.tile([P, 2, 3 * C], BF16, name="w1_sb")
+        pr = const.tile([P, P], BF16, name="pr")
+        nc.vector.memset(pr[:], 0.0)
+        x_v = [x[b].rearrange("(p j) t -> p j t", j=PACK) for b in range(B)]
+        nc.scalar.dma_start(out=pr[0:B * NQ, :], in_=mask.rearrange("b o (q r) -> (b o q) r", r=P))
+        nc.scalar.dma_start(out=pr[64:66, :], in_=g1.rearrange("(r f) -> r f", f=P))
+        nc.scalar.dma_start(out=pr[66:68, :], in_=be1.rearrange("(r f) -> r f", f=P))
+        nc.scalar.dma_start(out=pr[68:70, :], in_=b1.rearrange("(r f) -> r f", f=P))
+        for s in range(NCH):
+            nc.sync.dma_start(out=raw[0][:, :, s * CHUNK:(s + 1) * CHUNK],
+                              in_=x_v[0][:, :, s * CHUNK:(s + 1) * CHUNK])
+        nc.sync.dma_start(out=w1_sb[:], in_=w1.rearrange("(hh p) k -> p hh k", p=P))
+        for b in range(1, B):
+            nc.sync.dma_start(out=raw[b][:], in_=x_v[b])
+
+        ident_b = const.tile([P, P], BF16, name="ident_b")
+        make_identity(nc, ident_b[:])
+        ident_f = const.tile([P, P], F32, name="ident_f")
+        make_identity(nc, ident_f[:])
+        ones_f = const.tile([P, P], F32, name="ones_f")
+        nc.vector.memset(ones_f[:], 1.0)
+        half = const.tile([P, PACK], F32, name="half")
+        nc.vector.memset(half[:], 0.5)
+        nhalf = const.tile([P, TILES], F32, name="nhalf")
+        nc.vector.memset(nhalf[:], -0.5)
+        rhs_tot = const.tile([P, 32], F32, name="rhs_tot")
+        nc.vector.memset(rhs_tot[:], 0.0)
+
+        w1c = const.tile([P, 3, H], U32, name="w1c", align_bytes=64)
+        w1s = const.tile([P, 3, H], U8, name="w1s", align_bytes=64)
+        w1p = const.tile([P, 2, 3, PACK, P], BF16, name="w1p")
+        w1g = const.tile([P, 3, H, PACK], BF16, name="w1g", align_bytes=64)
+        cols = const.tile([P, 72], BF16, name="cols")
+        gb = const.tile([P, 4], F32, name="gb")
+        r_t = const.tile([P, B], F32, name="r_t")
+        b1bc = const.tile([P, H], BF16, name="b1bc")
+
+        def columns():
+            ps_pr = ps_ms.tile([P, P], BF16, tag="ms", name="ps_pr")
+            nc.tensor.transpose(out=ps_pr[:], in_=pr[:], identity=ident_b[:])
+            nc.vector.tensor_copy(out=cols[:, 0:70], in_=ps_pr[:, 0:70])
+            nc.vector.tensor_copy(out=gb[:], in_=ps_pr[:, 64:68])
+
+        def totals():
+            nc.vector.tensor_reduce(out=rhs_tot[:, 0:B], in_=cols[:, 0:B * NQ].rearrange("p (b q) -> p b q", b=B),
+                                    axis=AX.X, op=ALU.add)
+            ps_tot = ps_ms.tile([P, 32], F32, tag="ms", name="ps_tot")
+            nc.tensor.matmul(out=ps_tot[:], lhsT=ones_f[:], rhs=rhs_tot[:], start=True, stop=True)
+            rtot = const.tile([P, B], F32, name="rtot")
+            nc.vector.reciprocal(out=rtot[:], in_=ps_tot[:, 0:B])
+            nc.vector.tensor_scalar(out=r_t[:], in0=rtot[:], scalar1=float(T), scalar2=None, op0=ALU.mult)
+            ps_b1 = ps_ms.tile([P, H], BF16, tag="ms", name="ps_b1")
+            for hh in range(2):
+                nc.tensor.transpose(out=ps_b1[:, hh * P:(hh + 1) * P],
+                                    in_=cols[:, 68 + hh:69 + hh].to_broadcast([P, P]), identity=ident_b[:])
+            nc.vector.tensor_copy(out=b1bc[:], in_=ps_b1[:])
+
+        def w1_permute():
+            for hh in range(2):
+                nc.scalar.copy(out=w1p[:, hh], in_=w1_sb[:, hh, :].rearrange("p (g q j) -> p g j q", g=3, j=PACK))
+
+        def w1_transpose():
+            for g in range(3):
+                pw = ps_tr.tile([P, PACK, H], BF16, tag="tr", name="pw")
+                for hh in range(2):
+                    for j in range(PACK):
+                        nc.tensor.transpose(out=pw[:, j, hh * P:(hh + 1) * P], in_=w1p[:, hh, g, j, :],
+                                            identity=ident_b[:])
+                nc.scalar.copy(out=w1g[:, g], in_=pw[:].rearrange("q j h -> q h j"))
+
+        def w1_quant():
+            for g in range(3):
+                nc.vector.quantize_mx(out=w1c[:, g, :].bitcast(FP8X4), scales=w1s[:, g, :],
+                                      in_=w1g[:, g].rearrange("q h j -> q (h j)"))
+
+        xc = {}
+        xs = {}
+        st = {}
+        vb = {}
+        gr = {}
+        mk = {}
+        fin = {}
+
+        def mask_bc(f):
+            b, s = divmod(f, NCH)
+            pmk = ps_mk.tile([P, CHUNK], BF16, name="pmk")
+            for k in range(TILES):
+                c = b * NQ + s * TILES + k
+                nc.tensor.transpose(out=pmk[:, k * P:(k + 1) * P], in_=cols[:, c:c + 1].to_broadcast([P, P]),
+                                    identity=ident_b[:])
+            mk[f] = pmk
+
+        def tt_bn(f, between):
+            b, s = divmod(f, NCH)
+            cols_f = slice(s * CHUNK, (s + 1) * CHUNK)
+            if s == 0:
+                st[b] = per.tile([P, PACK, NCH, 6], F32, name="st")
+            xm = xmp.tile([P, PACK, CHUNK], BF16, name="xm")
+            nc.vector.tensor_tensor(out=xm[:], in0=raw[b][:, :, cols_f],
+                                    in1=mk.pop(f)[:].unsqueeze(1).to_broadcast([P, PACK, CHUNK]), op=ALU.mult)
+            if f + 1 < NG:
+                mask_bc(f + 1)
+            for j in range(PACK):
+                if j < len(between):
+                    between[j]()
+                nc.vector.bn_stats(out=st[b][:, j, s, :], in_=xm[:, j, :])
+
+        def regroup(f):
+            b, s = divmod(f, NCH)
+            cols_f = slice(s * CHUNK, (s + 1) * CHUNK)
+            grouped = grp.tile([P, CHUNK, PACK], BF16, name="grouped", align_bytes=64)
+            nc.scalar.copy(out=grouped[:].rearrange("p (c i) j -> p c j i", i=4),
+                           in_=raw[b][:, :, cols_f].rearrange("p j (c i) -> p c j i", i=4))
+            gr[f] = grouped
+
+        def quant(f):
+            b, s = divmod(f, NCH)
+            cols_f = slice(s * CHUNK, (s + 1) * CHUNK)
+            if s == 0:
+                xc[b] = cod.tile([P, T], U32, name="xc", align_bytes=64)
+                xs[b] = cod.tile([P, T], U8, name="xs", align_bytes=64)
+            nc.vector.quantize_mx(out=xc[b][:, cols_f].bitcast(FP8X4), scales=xs[b][:, cols_f],
+                                  in_=gr.pop(f)[:].rearrange("p w j -> p (w j)"))
+
+        def aggr(b):
+            mv = per.tile([P, PACK, 2], F32, name="mv")
+            for j in range(PACK):
+                nc.vector.bn_aggr(out=mv[:, j, :], in_=st[b][:, j].rearrange("p s k -> p (s k)"))
+            fin[b] = {"mv": mv}
+
+        def stat_ops(b):
+            e = fin[b]
+            mean = e["mv"][:, :, 0]
+            var = e["mv"][:, :, 1]
+            rb = r_t[:, b:b + 1]
+            m0 = per.tile([P, PACK], F32, name="m0")
+            d = per.tile([P, PACK], F32, name="d")
+            v0 = per.tile([P, PACK], F32, name="v0")
+            e["m0"] = m0
+            e["v0"] = v0
+            return [
+                lambda: nc.vector.tensor_scalar(out=m0[:], in0=mean, scalar1=rb, scalar2=None, op0=ALU.mult),
+                lambda: nc.vector.tensor_tensor(out=d[:], in0=mean, in1=m0[:], op=ALU.subtract),
+                lambda: nc.vector.tensor_tensor(out=d[:], in0=m0[:], in1=d[:], op=ALU.mult),
+                lambda: nc.vector.scalar_tensor_tensor(out=v0[:], in0=var, scalar=rb, in1=d[:],
+                                                       op0=ALU.mult, op1=ALU.add),
+            ]
+
+        def spread(b, gi, src):
+            e = fin[b]
+            msb = per.tile([P, P, PACK], BF16, name="msb%d" % gi, align_bytes=64)
+            if b < B - 1:
+                nc.gpsimd.tensor_scalar(out=msb[:], in0=src[:].unsqueeze(1).to_broadcast([P, P, PACK]),
+                                        scalar1=1.0, scalar2=0.0, op0=ALU.mult, op1=ALU.add)
+            else:
+                nc.vector.tensor_copy(out=msb[:], in_=src[:].unsqueeze(1).to_broadcast([P, P, PACK]))
+            e["msb%d" % gi] = msb
+
+        def spread_q(b, gi):
+            e = fin[b]
+            msb = e["msb%d" % gi]
+            mc = per.tile([P, P], U32, name="mc%d" % gi, align_bytes=64)
+            msc = per.tile([P, P], U8, name="msc%d" % gi, align_bytes=64)
+            nc.vector.quantize_mx(out=mc[:].bitcast(FP8X4), scales=msc[:], in_=msb[:].rearrange("p w j -> p (w j)"))
+            if gi == 0:
+                e["ps"] = ps_ms.tile([P, H], F32, tag="ms", name="ps_vb")
+            nc.tensor.matmul_mx(out=e["ps"][:], lhsT=mc[:].bitcast(FP8X4), lhsT_scale=msc[:],
+                                rhs=w1c[:, 1 + gi, :].bitcast(FP8X4), rhs_scale=w1s[:, 1 + gi, :],
+                                start=(gi == 0), stop=(gi == 1))
+
+        def stat_tail(b):
+            e = fin[b]
+            nc.vector.tensor_scalar(out=e["v0"][:], in0=e["v0"][:], scalar1=EPS_STD, scalar2=None, op0=ALU.max)
+            std = per.tile([P, PACK], F32, name="std")
+            nc.gpsimd.tensor_tensor(out=std[:], in0=e["v0"][:], in1=half[:], op=ALU.pow)
+            e["std"] = std
+            spread(b, 0, e["m0"])
+            if b < B - 1:
+                spread(b, 1, std)
+            else:
+                spread_q(b, 0)
+
+        def vb_add(b):
+            vb[b] = per.tile([P, H], F32, name="vb")
+            nc.vector.tensor_tensor(out=vb[b][:], in0=fin.pop(b)["ps"][:], in1=b1bc[:], op=ALU.add)
+
+        pss = {}
+        av = {}
+        sums = {}
+        nrm = {}
+        zhs = {}
+        pts = {}
+
+        def mx(g):
+            b, s = divmod(g, NCH)
+            pss[g] = []
+            for pair in range(TILES // 2):
+                ps = ps_mx.tile([P, 2, H], F32, name="ps")
+                for i in range(2):
+                    t0 = s * CHUNK + (2 * pair + i) * P
+                    nc.tensor.matmul_mx(out=ps[:, i, :], lhsT=xc[b][:, t0:t0 + P].bitcast(FP8X4),
+                                        lhsT_scale=xs[b][:, t0:t0 + P],
+                                        rhs=w1c[:, 0, :].bitcast(FP8X4), rhs_scale=w1s[:, 0, :],
+                                        start=True, stop=True)
+                pss[g].append(ps)
+
+        def p1(g):
+            b = g // NCH
+            a = up.tile([P, TILES, H], F32, name="a")
+            for pair in range(TILES // 2):
+                nc.vector.tensor_tensor(out=a[:, 2 * pair:2 * pair + 2, :], in0=pss[g][pair][:],
+                                        in1=vb[b][:].unsqueeze(1).to_broadcast([P, 2, H]), op=ALU.add)
+            pss.pop(g)
+            av[g] = a
+            if g in VSQ:
+                s2v = sml.tile([P, TILES], F32, name="s2v")
+                for k in range(TILES):
+                    junkv = zp.tile([P, H], F32, name="junkv")
+                    nc.vector.scalar_tensor_tensor(out=junkv[:], in0=a[:, k, :], scalar=0.0, in1=a[:, k, :],
+                                                   op0=ALU.max, op1=ALU.mult, accum_out=s2v[:, k:k + 1])
+                sums[(g, 1)] = s2v
+
+        def relu(g):
+            a = av[g]
+            s1 = sml.tile([P, TILES], F32, name="s1")
+            for k in range(TILES):
+                nc.scalar.activation(out=a[:, k, :], in_=a[:, k, :], func=ACT.Relu, accum_out=s1[:, k:k + 1])
+            sums[g] = s1
+
+        def variance_s(g):
+            a = av[g]
+            negmu = sml.tile([P, TILES], F32, name="negmu")
+            nc.scalar.activation(out=negmu[:], in_=sums.pop(g)[:], func=ACT.Copy, scale=-1.0 / H)
+            nrm[g] = negmu
+            if g not in VSQ:
+                s2s = sml.tile([P, TILES], F32, name="s2s")
+                for k in range(TILES):
+                    junk = zp.tile([P, H], F32, name="junk")
+                    nc.scalar.activation(out=junk[:], in_=a[:, k, :], func=ACT.Square, bias=negmu[:, k:k + 1],
+                                         accum_out=s2s[:, k:k + 1])
+                ve = sml.tile([P, TILES], F32, name="ve")
+                nc.scalar.activation(out=ve[:], in_=s2s[:], func=ACT.Copy, scale=1.0 / H, bias=EPS_LN)
+                rsqrt(g, ve)
+
+        def variance_v(g):
+            negmu = nrm[g]
+            msq = sml.tile([P, TILES], F32, name="msq")
+            vev = sml.tile([P, TILES], F32, name="vev")
+            nc.vector.tensor_tensor(out=msq[:], in0=negmu[:], in1=negmu[:], op=ALU.mult)
+            nc.vector.scalar_tensor_tensor(out=vev[:], in0=sums.pop((g, 1))[:], scalar=1.0 / H, in1=msq[:],
+                                           op0=ALU.mult, op1=ALU.subtract)
+            nc.vector.tensor_scalar(out=vev[:], in0=vev[:], scalar1=0.0, scalar2=EPS_LN, op0=ALU.max, op1=ALU.add)
+            rsqrt(g, vev)
+
+        def rsqrt(g, ve):
+            rstd = sml.tile([P, TILES], F32, name="rstd")
+            nc.gpsimd.tensor_tensor(out=rstd[:], in0=ve[:], in1=nhalf[:], op=ALU.pow)
+            nrm[g] = (nrm[g], rstd)
+            if g < P4V_FROM:
+                normalise(g, nc.gpsimd)
+
+        def normalise(g, eng):
+            a = av.pop(g)
+            negmu, rstd = nrm.pop(g)
+            zh = zp.tile([P, TILES, H], F32, name="zh")
+            for k in range(TILES):
+                eng.tensor_scalar(out=zh[:, k, :], in0=a[:, k, :], scalar1=negmu[:, k:k + 1],
+                                  scalar2=rstd[:, k:k + 1], op0=ALU.add, op1=ALU.mult)
+            zhs[g] = zh
+
+        def p4(g):
+            zh = zhs.pop(g)
+            pts[g] = []
+            for hh in range(2):
+                pt = ps_tr.tile([P, CHUNK], F32, tag="tr", name="pt")
+                for k in range(TILES):
+                    nc.tensor.transpose(out=pt[:, k * P:(k + 1) * P], in_=zh[:, k, hh * P:(hh + 1) * P],
+                                        identity=ident_f[:])
+                pts[g].append(pt)
+
+        def tanh_store(g):
+            b, s = divmod(g, NCH)
+            o = op.tile([P, 2, CHUNK], F32, name="o")
+            for hh in range(2):
+                nc.scalar.activation(out=o[:, hh, :], in_=pts[g][hh][:], func=ACT.Tanh,
+                                     scale=gb[:, hh:hh + 1], bias=gb[:, 2 + hh:3 + hh])
+                if g == NG - 1:
+                    nc.sync.dma_start(out=out[b][hh * P:(hh + 1) * P, s * CHUNK:(s + 1) * CHUNK], in_=o[:, hh, :])
+            pts.pop(g)
+            if g < NG - 1:
+                nc.sync.dma_start(out=out[b].rearrange("(hh p) t -> p hh t", p=P)[:, :, s * CHUNK:(s + 1) * CHUNK],
+                                  in_=o[:])
+
+        def ok(g):
+            return 0 <= g < NG
+
+        def closed(f, k):
+            return (f - k) // NCH if ok(f - k) and (f - k) % NCH == NCH - 1 else -1
+
+        columns()
+        mask_bc(0)
+        done = {"rg": 0, "q": 0}
+        rg_step = {}
+        for i in range(-LEAD, NG + P4O + 2):
+            f = i + LEAD
+            b_1 = closed(f, 1)
+            between = stat_ops(b_1) if b_1 >= 0 else []
+            if 0 <= closed(f, 2) < B - 1:
+                b_2 = closed(f, 2)
+                between = [lambda: None, lambda: None, lambda: spread_q(b_2, 0), lambda: spread_q(b_2, 1)]
+            if ok(f):
+                tt_bn(f, between)
+            else:
+                for fn in between:
+                    fn()
+            if b_1 >= 0:
+                stat_tail(b_1)
+            if f == 1:
+                totals()
+            if closed(f, 0) >= 0:
+                aggr(closed(f, 0))
+            if ok(i + 1):
+                mx(i + 1)
+            if closed(f, BCS_AT + 1) >= 0:
+                vb_add(closed(f, BCS_AT + 1))
+            if ok(i):
+                p1(i)
+            if ok(i - 2) and (i - 2) in VSQ:
+                variance_v(i - 2)
+            if ok(i - 2) and i - 2 >= P4V_FROM:
+                normalise(i - 2, nc.vector)
+            if f == 3:
+                w1_quant()
+            while done["q"] < done["rg"] and rg_step[done["q"]] < i:
+                quant(done["q"])
+                done["q"] = done["q"] + 1
+            if b_1 == B - 1:
+                spread(b_1, 1, fin[b_1]["std"])
+                spread_q(b_1, 1)
+            if ok(i - 1):
+                relu(i - 1)
+                variance_s(i - 1)
+            if ok(i - P4O):
+                p4(i - P4O)
+            if f == 1:
+                w1_permute()
+            if f == 2:
+                w1_transpose()
+            while done["rg"] <= min(NG - 1, f + RGA):
+                regroup(done["rg"])
+                rg_step[done["rg"]] = i
+                done["rg"] = done["rg"] + 1
+            if ok(i - P4O - 1):
+                tanh_store(i - P4O - 1)

@@ -23,11 +23,9 @@ NQ = T // P
 EPS_LN = 1e-5
 EPS_STD = 1e-5
 LEAD = 5
-P4O = 2
 RGA = 3
-P4V_FROM = 12
-BCS_AT = 1
-VSQ = [14,15]
+VNORM_FROM = 10
+VROUTE = [13, 15]
 FLOPS = 2 * B * H * 3 * C * T
 
 
@@ -52,16 +50,18 @@ def tile_attentivestatspool_pa_t_kernel(tc, x, mask, w1, b1, g1, be1, out):
         raw = [const.tile([P, PACK, T], BF16, name="raw%d" % b) for b in range(B)]
         w1_sb = const.tile([P, 2, 3 * C], BF16, name="w1_sb")
         pr = const.tile([P, P], BF16, name="pr")
-        nc.vector.memset(pr[:], 0.0)
+        prm = const.tile([P, P], BF16, name="prm")
         x_v = [x[b].rearrange("(p j) t -> p j t", j=PACK) for b in range(B)]
         nc.scalar.dma_start(out=pr[0:B * NQ, :], in_=mask.rearrange("b o (q r) -> (b o q) r", r=P))
-        nc.scalar.dma_start(out=pr[64:66, :], in_=g1.rearrange("(r f) -> r f", f=P))
-        nc.scalar.dma_start(out=pr[66:68, :], in_=be1.rearrange("(r f) -> r f", f=P))
-        nc.scalar.dma_start(out=pr[68:70, :], in_=b1.rearrange("(r f) -> r f", f=P))
+        nc.vector.memset(pr[B * NQ:P, :], 0.0)
+        nc.vector.memset(prm[:], 0.0)
         for s in range(NCH):
             nc.sync.dma_start(out=raw[0][:, :, s * CHUNK:(s + 1) * CHUNK],
                               in_=x_v[0][:, :, s * CHUNK:(s + 1) * CHUNK])
         nc.sync.dma_start(out=w1_sb[:], in_=w1.rearrange("(hh p) k -> p hh k", p=P))
+        nc.sync.dma_start(out=prm[0:2, :], in_=g1.rearrange("(r f) -> r f", f=P))
+        nc.sync.dma_start(out=prm[2:4, :], in_=be1.rearrange("(r f) -> r f", f=P))
+        nc.sync.dma_start(out=prm[4:6, :], in_=b1.rearrange("(r f) -> r f", f=P))
         for b in range(1, B):
             nc.sync.dma_start(out=raw[b][:], in_=x_v[b])
 
@@ -69,56 +69,63 @@ def tile_attentivestatspool_pa_t_kernel(tc, x, mask, w1, b1, g1, be1, out):
         make_identity(nc, ident_b[:])
         ident_f = const.tile([P, P], F32, name="ident_f")
         make_identity(nc, ident_f[:])
-        ones_f = const.tile([P, P], F32, name="ones_f")
-        nc.vector.memset(ones_f[:], 1.0)
+        warm = const.tile([P, 1], F32, name="warm")
+        nc.vector.memset(warm[:], 0.0)
+        nc.scalar.activation(out=warm[:], in_=warm[:], func=ACT.Tanh)
+        ones_t = const.tile([P, P], BF16, name="ones_t")
+        nc.vector.memset(ones_t[:], 1.0 / T)
         half = const.tile([P, PACK], F32, name="half")
         nc.vector.memset(half[:], 0.5)
         nhalf = const.tile([P, TILES], F32, name="nhalf")
         nc.vector.memset(nhalf[:], -0.5)
-        rhs_tot = const.tile([P, 32], F32, name="rhs_tot")
-        nc.vector.memset(rhs_tot[:], 0.0)
 
         w1c = const.tile([P, 3, H], U32, name="w1c", align_bytes=64)
         w1s = const.tile([P, 3, H], U8, name="w1s", align_bytes=64)
-        w1p = const.tile([P, 2, 3, PACK, P], BF16, name="w1p")
         w1g = const.tile([P, 3, H, PACK], BF16, name="w1g", align_bytes=64)
-        cols = const.tile([P, 72], BF16, name="cols")
+        cols = const.tile([P, B * NQ], BF16, name="cols")
         gb = const.tile([P, 4], F32, name="gb")
+        b1c = const.tile([P, 2], BF16, name="b1c")
         r_t = const.tile([P, B], F32, name="r_t")
         b1bc = const.tile([P, H], BF16, name="b1bc")
 
         def columns():
             ps_pr = ps_ms.tile([P, P], BF16, tag="ms", name="ps_pr")
             nc.tensor.transpose(out=ps_pr[:], in_=pr[:], identity=ident_b[:])
-            nc.vector.tensor_copy(out=cols[:, 0:70], in_=ps_pr[:, 0:70])
-            nc.vector.tensor_copy(out=gb[:], in_=ps_pr[:, 64:68])
+            nc.vector.tensor_copy(out=cols[:], in_=ps_pr[:, 0:B * NQ])
 
-        def totals():
-            nc.vector.tensor_reduce(out=rhs_tot[:, 0:B], in_=cols[:, 0:B * NQ].rearrange("p (b q) -> p b q", b=B),
-                                    axis=AX.X, op=ALU.add)
-            ps_tot = ps_ms.tile([P, 32], F32, tag="ms", name="ps_tot")
-            nc.tensor.matmul(out=ps_tot[:], lhsT=ones_f[:], rhs=rhs_tot[:], start=True, stop=True)
-            rtot = const.tile([P, B], F32, name="rtot")
-            nc.vector.reciprocal(out=rtot[:], in_=ps_tot[:, 0:B])
-            nc.vector.tensor_scalar(out=r_t[:], in0=rtot[:], scalar1=float(T), scalar2=None, op0=ALU.mult)
+        def totals_mm():
+            ps_tot = ps_ms.tile([P, B * NQ], F32, tag="ms", name="ps_tot")
+            nc.tensor.matmul(out=ps_tot[:], lhsT=ones_t[:], rhs=cols[:], start=True, stop=True)
+            return ps_tot
+
+        def totals(ps_tot):
+            tot = const.tile([P, B], F32, name="tot")
+            nc.vector.tensor_reduce(out=tot[:], in_=ps_tot[:].rearrange("p (b q) -> p b q", b=B), axis=AX.X, op=ALU.add)
+            nc.vector.reciprocal(out=r_t[:], in_=tot[:])
+
+        def params():
+            ps_par = ps_ms.tile([P, P], BF16, tag="ms", name="ps_par")
+            nc.tensor.transpose(out=ps_par[:], in_=prm[:], identity=ident_b[:])
+            nc.scalar.copy(out=gb[:], in_=ps_par[:, 0:4])
+            nc.scalar.copy(out=b1c[:], in_=ps_par[:, 4:6])
+
+        def params_b1():
             ps_b1 = ps_ms.tile([P, H], BF16, tag="ms", name="ps_b1")
             for hh in range(2):
                 nc.tensor.transpose(out=ps_b1[:, hh * P:(hh + 1) * P],
-                                    in_=cols[:, 68 + hh:69 + hh].to_broadcast([P, P]), identity=ident_b[:])
-            nc.vector.tensor_copy(out=b1bc[:], in_=ps_b1[:])
-
-        def w1_permute():
-            for hh in range(2):
-                nc.scalar.copy(out=w1p[:, hh], in_=w1_sb[:, hh, :].rearrange("p (g q j) -> p g j q", g=3, j=PACK))
+                                    in_=b1c[:, hh:hh + 1].to_broadcast([P, P]), identity=ident_b[:])
+            nc.scalar.copy(out=b1bc[:], in_=ps_b1[:])
 
         def w1_transpose():
+            words = w1_sb[:].rearrange("p hh k -> p (hh k)").bitcast(F32)
             for g in range(3):
-                pw = ps_tr.tile([P, PACK, H], BF16, tag="tr", name="pw")
-                for hh in range(2):
-                    for j in range(PACK):
-                        nc.tensor.transpose(out=pw[:, j, hh * P:(hh + 1) * P], in_=w1p[:, hh, g, j, :],
-                                            identity=ident_b[:])
-                nc.scalar.copy(out=w1g[:, g], in_=pw[:].rearrange("q j h -> q h j"))
+                pw = ps_tr.tile([P, 2, H], F32, tag="tr", name="pw")
+                for u in range(2):
+                    for hh in range(2):
+                        w0 = hh * (3 * C // 2) + g * (C // 2)
+                        nc.tensor.transpose(out=pw[:, u, hh * P:(hh + 1) * P], in_=words[:, w0 + u:w0 + C // 2:2],
+                                            identity=ident_f[:])
+                nc.scalar.copy(out=w1g[:, g].bitcast(F32), in_=pw[:].rearrange("q u h -> q h u"))
 
         def w1_quant():
             for g in range(3):
@@ -128,7 +135,7 @@ def tile_attentivestatspool_pa_t_kernel(tc, x, mask, w1, b1, g1, be1, out):
         xc = {}
         xs = {}
         st = {}
-        vb = {}
+        rows = {}
         gr = {}
         mk = {}
         fin = {}
@@ -138,24 +145,28 @@ def tile_attentivestatspool_pa_t_kernel(tc, x, mask, w1, b1, g1, be1, out):
             pmk = ps_mk.tile([P, CHUNK], BF16, name="pmk")
             for k in range(TILES):
                 c = b * NQ + s * TILES + k
-                nc.tensor.transpose(out=pmk[:, k * P:(k + 1) * P], in_=cols[:, c:c + 1].to_broadcast([P, P]),
-                                    identity=ident_b[:])
+                if f == 0:
+                    nc.tensor.matmul(out=pmk[:, k * P:(k + 1) * P], lhsT=ident_b[:, c:c + 1].to_broadcast([P, P]),
+                                     rhs=pr[:], start=True, stop=True)
+                else:
+                    nc.tensor.transpose(out=pmk[:, k * P:(k + 1) * P], in_=cols[:, c:c + 1].to_broadcast([P, P]),
+                                        identity=ident_b[:])
             mk[f] = pmk
 
-        def tt_bn(f, between):
+        xms = {}
+
+        def mask_mul(f):
             b, s = divmod(f, NCH)
-            cols_f = slice(s * CHUNK, (s + 1) * CHUNK)
-            if s == 0:
-                st[b] = per.tile([P, PACK, NCH, 6], F32, name="st")
             xm = xmp.tile([P, PACK, CHUNK], BF16, name="xm")
-            nc.vector.tensor_tensor(out=xm[:], in0=raw[b][:, :, cols_f],
+            nc.vector.tensor_tensor(out=xm[:], in0=raw[b][:, :, s * CHUNK:(s + 1) * CHUNK],
                                     in1=mk.pop(f)[:].unsqueeze(1).to_broadcast([P, PACK, CHUNK]), op=ALU.mult)
-            if f + 1 < NG:
-                mask_bc(f + 1)
-            for j in range(PACK):
-                if j < len(between):
-                    between[j]()
-                nc.vector.bn_stats(out=st[b][:, j, s, :], in_=xm[:, j, :])
+            xms[f] = xm
+
+        def bn(f, j):
+            b, s = divmod(f, NCH)
+            if s == 0 and j == 0:
+                st[b] = per.tile([P, PACK, NCH, 6], F32, name="st")
+            nc.vector.bn_stats(out=st[b][:, j, s, :], in_=xms[f][:, j, :])
 
         def regroup(f):
             b, s = divmod(f, NCH)
@@ -174,11 +185,10 @@ def tile_attentivestatspool_pa_t_kernel(tc, x, mask, w1, b1, g1, be1, out):
             nc.vector.quantize_mx(out=xc[b][:, cols_f].bitcast(FP8X4), scales=xs[b][:, cols_f],
                                   in_=gr.pop(f)[:].rearrange("p w j -> p (w j)"))
 
-        def aggr(b):
-            mv = per.tile([P, PACK, 2], F32, name="mv")
-            for j in range(PACK):
-                nc.vector.bn_aggr(out=mv[:, j, :], in_=st[b][:, j].rearrange("p s k -> p (s k)"))
-            fin[b] = {"mv": mv}
+        def aggr(b, j):
+            if j == 0:
+                fin[b] = {"mv": per.tile([P, PACK, 2], F32, name="mv")}
+            nc.vector.bn_aggr(out=fin[b]["mv"][:, j, :], in_=st[b][:, j].rearrange("p s k -> p (s k)"))
 
         def stat_ops(b):
             e = fin[b]
@@ -190,12 +200,28 @@ def tile_attentivestatspool_pa_t_kernel(tc, x, mask, w1, b1, g1, be1, out):
             v0 = per.tile([P, PACK], F32, name="v0")
             e["m0"] = m0
             e["v0"] = v0
+            on_g = b < B - 1
+
+            def first():
+                nc.vector.tensor_scalar(out=m0[:], in0=mean, scalar1=rb, scalar2=None, op0=ALU.mult)
+                if on_g:
+                    spread(b, 0, m0)
+
+            def last():
+                nc.vector.tensor_scalar(out=v0[:], in0=v0[:], scalar1=EPS_STD, scalar2=None, op0=ALU.max)
+                std = per.tile([P, PACK], F32, name="std")
+                nc.gpsimd.tensor_tensor(out=std[:], in0=v0[:], in1=half[:], op=ALU.pow)
+                e["std"] = std
+                if on_g:
+                    spread(b, 1, std)
+
             return [
-                lambda: nc.vector.tensor_scalar(out=m0[:], in0=mean, scalar1=rb, scalar2=None, op0=ALU.mult),
+                first,
                 lambda: nc.vector.tensor_tensor(out=d[:], in0=mean, in1=m0[:], op=ALU.subtract),
                 lambda: nc.vector.tensor_tensor(out=d[:], in0=m0[:], in1=d[:], op=ALU.mult),
                 lambda: nc.vector.scalar_tensor_tensor(out=v0[:], in0=var, scalar=rb, in1=d[:],
                                                        op0=ALU.mult, op1=ALU.add),
+                last,
             ]
 
         def spread(b, gi, src):
@@ -214,31 +240,11 @@ def tile_attentivestatspool_pa_t_kernel(tc, x, mask, w1, b1, g1, be1, out):
             mc = per.tile([P, P], U32, name="mc%d" % gi, align_bytes=64)
             msc = per.tile([P, P], U8, name="msc%d" % gi, align_bytes=64)
             nc.vector.quantize_mx(out=mc[:].bitcast(FP8X4), scales=msc[:], in_=msb[:].rearrange("p w j -> p (w j)"))
-            if gi == 0:
-                e["ps"] = ps_ms.tile([P, H], F32, tag="ms", name="ps_vb")
-            nc.tensor.matmul_mx(out=e["ps"][:], lhsT=mc[:].bitcast(FP8X4), lhsT_scale=msc[:],
-                                rhs=w1c[:, 1 + gi, :].bitcast(FP8X4), rhs_scale=w1s[:, 1 + gi, :],
-                                start=(gi == 0), stop=(gi == 1))
-
-        def stat_tail(b):
-            e = fin[b]
-            nc.vector.tensor_scalar(out=e["v0"][:], in0=e["v0"][:], scalar1=EPS_STD, scalar2=None, op0=ALU.max)
-            std = per.tile([P, PACK], F32, name="std")
-            nc.gpsimd.tensor_tensor(out=std[:], in0=e["v0"][:], in1=half[:], op=ALU.pow)
-            e["std"] = std
-            spread(b, 0, e["m0"])
-            if b < B - 1:
-                spread(b, 1, std)
-            else:
-                spread_q(b, 0)
-
-        def vb_add(b):
-            vb[b] = per.tile([P, H], F32, name="vb")
-            nc.vector.tensor_tensor(out=vb[b][:], in0=fin.pop(b)["ps"][:], in1=b1bc[:], op=ALU.add)
+            rows[(b, gi)] = (mc, msc)
 
         pss = {}
         av = {}
-        sums = {}
+        ln = {}
         nrm = {}
         zhs = {}
         pts = {}
@@ -250,74 +256,73 @@ def tile_attentivestatspool_pa_t_kernel(tc, x, mask, w1, b1, g1, be1, out):
                 ps = ps_mx.tile([P, 2, H], F32, name="ps")
                 for i in range(2):
                     t0 = s * CHUNK + (2 * pair + i) * P
-                    nc.tensor.matmul_mx(out=ps[:, i, :], lhsT=xc[b][:, t0:t0 + P].bitcast(FP8X4),
-                                        lhsT_scale=xs[b][:, t0:t0 + P],
-                                        rhs=w1c[:, 0, :].bitcast(FP8X4), rhs_scale=w1s[:, 0, :],
-                                        start=True, stop=True)
+                    stat = [(xc[b][:, t0:t0 + P], xs[b][:, t0:t0 + P])]
+                    stat += [(rows[(b, gi)][0][:], rows[(b, gi)][1][:]) for gi in range(2)]
+                    for n in range(3):
+                        nc.tensor.matmul_mx(out=ps[:, i, :], lhsT=stat[n][0].bitcast(FP8X4), lhsT_scale=stat[n][1],
+                                            rhs=w1c[:, n, :].bitcast(FP8X4), rhs_scale=w1s[:, n, :],
+                                            start=(n == 0), stop=(n == 2))
                 pss[g].append(ps)
 
         def p1(g):
-            b = g // NCH
             a = up.tile([P, TILES, H], F32, name="a")
             for pair in range(TILES // 2):
                 nc.vector.tensor_tensor(out=a[:, 2 * pair:2 * pair + 2, :], in0=pss[g][pair][:],
-                                        in1=vb[b][:].unsqueeze(1).to_broadcast([P, 2, H]), op=ALU.add)
+                                        in1=b1bc[:].unsqueeze(1).to_broadcast([P, 2, H]), op=ALU.add)
             pss.pop(g)
             av[g] = a
-            if g in VSQ:
-                s2v = sml.tile([P, TILES], F32, name="s2v")
-                for k in range(TILES):
-                    junkv = zp.tile([P, H], F32, name="junkv")
-                    nc.vector.scalar_tensor_tensor(out=junkv[:], in0=a[:, k, :], scalar=0.0, in1=a[:, k, :],
-                                                   op0=ALU.max, op1=ALU.mult, accum_out=s2v[:, k:k + 1])
-                sums[(g, 1)] = s2v
 
-        def relu(g):
+        def relu_square(g):
             a = av[g]
-            s1 = sml.tile([P, TILES], F32, name="s1")
+            mu = sml.tile([P, TILES], F32, name="mu")
             for k in range(TILES):
-                nc.scalar.activation(out=a[:, k, :], in_=a[:, k, :], func=ACT.Relu, accum_out=s1[:, k:k + 1])
-            sums[g] = s1
+                nc.scalar.activation(out=a[:, k, :], in_=a[:, k, :], func=ACT.Relu, scale=1.0 / H,
+                                     accum_out=mu[:, k:k + 1])
+            sq = sml.tile([P, TILES], F32, name="sq")
+            for k in range(TILES):
+                junk = zp.tile([P, H], F32, name="junk")
+                nc.scalar.activation(out=junk[:], in_=a[:, k, :], func=ACT.Square, scale=-float(H),
+                                     bias=mu[:, k:k + 1], accum_out=sq[:, k:k + 1])
+            ln[g] = (mu, sq)
 
-        def variance_s(g):
-            a = av[g]
+        def norm_g(g):
+            mu, sq = ln.pop(g)
             negmu = sml.tile([P, TILES], F32, name="negmu")
-            nc.scalar.activation(out=negmu[:], in_=sums.pop(g)[:], func=ACT.Copy, scale=-1.0 / H)
-            nrm[g] = negmu
-            if g not in VSQ:
-                s2s = sml.tile([P, TILES], F32, name="s2s")
-                for k in range(TILES):
-                    junk = zp.tile([P, H], F32, name="junk")
-                    nc.scalar.activation(out=junk[:], in_=a[:, k, :], func=ACT.Square, bias=negmu[:, k:k + 1],
-                                         accum_out=s2s[:, k:k + 1])
-                ve = sml.tile([P, TILES], F32, name="ve")
-                nc.scalar.activation(out=ve[:], in_=s2s[:], func=ACT.Copy, scale=1.0 / H, bias=EPS_LN)
-                rsqrt(g, ve)
-
-        def variance_v(g):
-            negmu = nrm[g]
-            msq = sml.tile([P, TILES], F32, name="msq")
-            vev = sml.tile([P, TILES], F32, name="vev")
-            nc.vector.tensor_tensor(out=msq[:], in0=negmu[:], in1=negmu[:], op=ALU.mult)
-            nc.vector.scalar_tensor_tensor(out=vev[:], in0=sums.pop((g, 1))[:], scalar=1.0 / H, in1=msq[:],
-                                           op0=ALU.mult, op1=ALU.subtract)
-            nc.vector.tensor_scalar(out=vev[:], in0=vev[:], scalar1=0.0, scalar2=EPS_LN, op0=ALU.max, op1=ALU.add)
-            rsqrt(g, vev)
-
-        def rsqrt(g, ve):
+            nc.gpsimd.tensor_scalar(out=negmu[:], in0=mu[:], scalar1=-1.0 / H, scalar2=0.0, op0=ALU.mult, op1=ALU.add)
+            ve = sml.tile([P, TILES], F32, name="ve")
+            nc.gpsimd.tensor_scalar(out=ve[:], in0=sq[:], scalar1=1.0 / H**3, scalar2=EPS_LN / H**2,
+                                    op0=ALU.mult, op1=ALU.add)
             rstd = sml.tile([P, TILES], F32, name="rstd")
             nc.gpsimd.tensor_tensor(out=rstd[:], in0=ve[:], in1=nhalf[:], op=ALU.pow)
-            nrm[g] = (nrm[g], rstd)
-            if g < P4V_FROM:
-                normalise(g, nc.gpsimd)
+            nrm[g] = [(negmu[:, k:k + 1], rstd[:, k:k + 1]) for k in range(TILES)]
+
+        def vroute(g):
+            a = av[g]
+            nc.vector.tensor_scalar(out=a[:], in0=a[:], scalar1=0.0, scalar2=None, op0=ALU.max)
+            st4 = sml.tile([P, TILES, 6], F32, name="st4")
+            mv4 = sml.tile([P, TILES, 2], F32, name="mv4")
+            for k in range(TILES):
+                nc.vector.bn_stats(out=st4[:, k, :], in_=a[:, k, :])
+            for k in range(TILES):
+                nc.vector.bn_aggr(out=mv4[:, k, :], in_=st4[:, k, :])
+            ln[g] = mv4
+
+        def norm_v(g):
+            mv4 = ln.pop(g)
+            ve = sml.tile([P, TILES], F32, name="ve")
+            nc.gpsimd.tensor_scalar(out=ve[:], in0=mv4[:, :, 1], scalar1=1.0, scalar2=EPS_LN,
+                                    op0=ALU.mult, op1=ALU.add)
+            rstd = sml.tile([P, TILES], F32, name="rstd")
+            nc.gpsimd.tensor_tensor(out=rstd[:], in0=ve[:], in1=nhalf[:], op=ALU.pow)
+            nrm[g] = [(mv4[:, k, 0:1], rstd[:, k:k + 1]) for k in range(TILES)]
 
         def normalise(g, eng):
             a = av.pop(g)
-            negmu, rstd = nrm.pop(g)
             zh = zp.tile([P, TILES, H], F32, name="zh")
             for k in range(TILES):
-                eng.tensor_scalar(out=zh[:, k, :], in0=a[:, k, :], scalar1=negmu[:, k:k + 1],
-                                  scalar2=rstd[:, k:k + 1], op0=ALU.add, op1=ALU.mult)
+                mean, rstd = nrm[g][k]
+                eng.tensor_scalar(out=zh[:, k, :], in0=a[:, k, :], scalar1=mean, scalar2=rstd,
+                                  op0=ALU.subtract if g in VROUTE else ALU.add, op1=ALU.mult)
             zhs[g] = zh
 
         def p4(g):
@@ -346,61 +351,135 @@ def tile_attentivestatspool_pa_t_kernel(tc, x, mask, w1, b1, g1, be1, out):
         def ok(g):
             return 0 <= g < NG
 
-        def closed(f, k):
-            return (f - k) // NCH if ok(f - k) and (f - k) % NCH == NCH - 1 else -1
-
-        columns()
-        mask_bc(0)
         done = {"rg": 0, "q": 0}
-        rg_step = {}
-        for i in range(-LEAD, NG + P4O + 2):
-            f = i + LEAD
-            b_1 = closed(f, 1)
-            between = stat_ops(b_1) if b_1 >= 0 else []
-            if 0 <= closed(f, 2) < B - 1:
-                b_2 = closed(f, 2)
-                between = [lambda: None, lambda: None, lambda: spread_q(b_2, 0), lambda: spread_q(b_2, 1)]
-            if ok(f):
-                tt_bn(f, between)
-            else:
-                for fn in between:
-                    fn()
-            if b_1 >= 0:
-                stat_tail(b_1)
-            if f == 1:
-                totals()
-            if closed(f, 0) >= 0:
-                aggr(closed(f, 0))
-            if ok(i + 1):
-                mx(i + 1)
-            if closed(f, BCS_AT + 1) >= 0:
-                vb_add(closed(f, BCS_AT + 1))
-            if ok(i):
-                p1(i)
-            if ok(i - 2) and (i - 2) in VSQ:
-                variance_v(i - 2)
-            if ok(i - 2) and i - 2 >= P4V_FROM:
-                normalise(i - 2, nc.vector)
-            if f == 3:
-                w1_quant()
-            while done["q"] < done["rg"] and rg_step[done["q"]] < i:
+
+        def regroup_to(n):
+            while done["rg"] < min(NG, n):
+                regroup(done["rg"])
+                done["rg"] = done["rg"] + 1
+
+        def quant_to(n):
+            while done["q"] < min(NG, n):
                 quant(done["q"])
                 done["q"] = done["q"] + 1
-            if b_1 == B - 1:
-                spread(b_1, 1, fin[b_1]["std"])
-                spread_q(b_1, 1)
-            if ok(i - 1):
-                relu(i - 1)
-                variance_s(i - 1)
-            if ok(i - P4O):
-                p4(i - P4O)
+
+        mask_bc(0)
+        mask_mul(0)
+        columns()
+        mask_bc(1)
+        regroup_to(RGA)
+        for f in range(NG):
+            i = f - LEAD
+            b, s = divmod(f, NCH)
+            slots = [[], [], [], [], []]
+            if s == NCH - 1:
+                slots[1].append(lambda b=b: aggr(b, 0))
+                slots[2].append(lambda b=b: aggr(b, 1))
+                slots[3].append(lambda b=b: aggr(b, 2))
+            if s == 0 and b > 0:
+                slots[0].append(lambda b=b: aggr(b - 1, 3))
+                ops = {}
+                for n in range(5):
+                    slots[n].append(lambda b=b, n=n: ops.setdefault("l", stat_ops(b - 1) if n == 0 else None)[n]())
+                slots[0], slots[1] = slots[0][:1], slots[0][1:] + slots[1]
+            if s == 1 and b > 0:
+                slots[1].append(lambda b=b: spread_q(b - 1, 0))
+                slots[2].append(lambda b=b: (spread_q(b - 1, 1), mx(NCH * (b - 1))))
             if f == 1:
-                w1_permute()
-            if f == 2:
+                ptot = totals_mm()
+                slots[2].append(lambda: totals(ptot))
+            if f == 3:
+                slots[3].append(w1_quant)
+            if ok(i - 2):
+                norm_g(i - 2)
+                normalise(i - 2, nc.gpsimd)
+            if ok(i - 1):
+                relu_square(i - 1)
+            if f == 1:
                 w1_transpose()
-            while done["rg"] <= min(NG - 1, f + RGA):
-                regroup(done["rg"])
-                rg_step[done["rg"]] = i
-                done["rg"] = done["rg"] + 1
-            if ok(i - P4O - 1):
-                tanh_store(i - P4O - 1)
+            if f == 2:
+                params()
+            if f == 3:
+                params_b1()
+            if ok(i - 3):
+                p4(i - 3)
+                tanh_store(i - 3)
+            regroup_to(f + 1 + RGA)
+            for j in range(PACK):
+                bn(f, j)
+                if j == 1 and f + 1 < NG:
+                    mask_mul(f + 1)
+                    if f + 2 < NG:
+                        mask_bc(f + 2)
+                for fn in slots[j]:
+                    fn()
+            for fn in slots[4]:
+                fn()
+            if f >= 3:
+                quant_to(f + 1 if f < NG - 4 else NG - 4)
+            if ok(i):
+                p1(i)
+            if ok(i) and (i + 1) % NCH:
+                mx(i + 1)
+        b = B - 1
+        last = NG - NCH
+        aggr(b, 3)
+        ops = stat_ops(b)
+        quant_to(last + 1)
+        ops[0]()
+        norm_g(last - 3)
+        quant_to(last + 2)
+        ops[1]()
+        spread(b, 0, fin[b]["m0"])
+        ops[2]()
+        spread_q(b, 0)
+        ops[3]()
+        quant_to(last + 3)
+        ops[4]()
+        relu_square(last - 2)
+        p4(last - 4)
+        tanh_store(last - 4)
+        normalise(last - 3, nc.vector)
+        p1(last - 1)
+        spread(b, 1, fin[b]["std"])
+        quant_to(last + 4)
+        spread_q(b, 1)
+        p4(last - 3)
+        mx(last)
+        norm_g(last - 2)
+        relu_square(last - 1)
+        tanh_store(last - 3)
+        normalise(last - 2, nc.vector)
+        p1(last)
+        mx(last + 1)
+        p1(last + 1)
+        mx(last + 2)
+        relu_square(last)
+        norm_g(last - 1)
+        p4(last - 2)
+        tanh_store(last - 2)
+        vroute(last + 1)
+        norm_v(last + 1)
+        normalise(last - 1, nc.vector)
+        norm_g(last)
+        p1(last + 2)
+        p4(last - 1)
+        mx(last + 3)
+        tanh_store(last - 1)
+        normalise(last, nc.vector)
+        normalise(last + 1, nc.vector)
+        p4(last)
+        relu_square(last + 2)
+        tanh_store(last)
+        p1(last + 3)
+        p4(last + 1)
+        vroute(last + 3)
+        norm_g(last + 2)
+        norm_v(last + 3)
+        tanh_store(last + 1)
+        normalise(last + 2, nc.vector)
+        p4(last + 2)
+        tanh_store(last + 2)
+        normalise(last + 3, nc.vector)
+        p4(last + 3)
+        tanh_store(last + 3)

@@ -24,6 +24,7 @@ EPS_LN = 1e-5
 EPS_STD = 1e-5
 LEAD = 5
 RGA = 3
+GMASK = [3, 5]
 VNORM_FROM = 10
 VROUTE = [13, 15]
 FLOPS = 2 * B * H * 3 * C * T
@@ -34,13 +35,14 @@ def tile_attentivestatspool_pa_t_kernel(tc, x, mask, w1, b1, g1, be1, out):
     with ExitStack() as ctx:
         const = ctx.enter_context(tc.tile_pool(name="const", bufs=1))
         xmp = ctx.enter_context(tc.tile_pool(name="xmp", bufs=3))
+        xmg = ctx.enter_context(tc.tile_pool(name="xmg", bufs=2))
         grp = ctx.enter_context(tc.tile_pool(name="grp", bufs=6))
         cod = ctx.enter_context(tc.tile_pool(name="cod", bufs=3))
         sml = ctx.enter_context(tc.tile_pool(name="sml", bufs=6))
         per = ctx.enter_context(tc.tile_pool(name="per", bufs=2))
         up = ctx.enter_context(tc.tile_pool(name="up", bufs=5))
         zp = ctx.enter_context(tc.tile_pool(name="zp", bufs=3))
-        op = ctx.enter_context(tc.tile_pool(name="op", bufs=3))
+        op = ctx.enter_context(tc.tile_pool(name="op", bufs=4))
         ps_mx = ctx.enter_context(tc.psum_pool(name="ps_mx", bufs=3))
         ps_tr = ctx.enter_context(tc.psum_pool(name="ps_tr", bufs=3))
         ps_ms = ctx.enter_context(tc.psum_pool(name="ps_ms", bufs=1))
@@ -55,7 +57,9 @@ def tile_attentivestatspool_pa_t_kernel(tc, x, mask, w1, b1, g1, be1, out):
         nc.scalar.dma_start(out=pr[0:B * NQ, :], in_=mask.rearrange("b o (q r) -> (b o q) r", r=P))
         nc.vector.memset(pr[B * NQ:P, :], 0.0)
         nc.vector.memset(prm[:], 0.0)
-        for s in range(NCH):
+        for j in (0, 2):
+            nc.sync.dma_start(out=raw[0][:, j:j + 2, 0:CHUNK], in_=x_v[0][:, j:j + 2, 0:CHUNK])
+        for s in range(1, NCH):
             nc.sync.dma_start(out=raw[0][:, :, s * CHUNK:(s + 1) * CHUNK],
                               in_=x_v[0][:, :, s * CHUNK:(s + 1) * CHUNK])
         nc.sync.dma_start(out=w1_sb[:], in_=w1.rearrange("(hh p) k -> p hh k", p=P))
@@ -63,7 +67,10 @@ def tile_attentivestatspool_pa_t_kernel(tc, x, mask, w1, b1, g1, be1, out):
         nc.sync.dma_start(out=prm[2:4, :], in_=be1.rearrange("(r f) -> r f", f=P))
         nc.sync.dma_start(out=prm[4:6, :], in_=b1.rearrange("(r f) -> r f", f=P))
         for b in range(1, B):
-            nc.sync.dma_start(out=raw[b][:], in_=x_v[b])
+            for s in range(0, NCH, NCH if b > 1 else 2):
+                n = NCH if b > 1 else 2
+                nc.sync.dma_start(out=raw[b][:, :, s * CHUNK:(s + n) * CHUNK],
+                                  in_=x_v[b][:, :, s * CHUNK:(s + n) * CHUNK])
 
         ident_b = const.tile([P, P], BF16, name="ident_b")
         make_identity(nc, ident_b[:])
@@ -142,10 +149,13 @@ def tile_attentivestatspool_pa_t_kernel(tc, x, mask, w1, b1, g1, be1, out):
 
         def mask_bc(f):
             b, s = divmod(f, NCH)
-            pmk = ps_mk.tile([P, CHUNK], BF16, name="pmk")
+            if f in GMASK:
+                pmk = ps_tr.tile([P, CHUNK], BF16, tag="tr", name="pmk2")
+            else:
+                pmk = ps_mk.tile([P, CHUNK], BF16, name="pmk")
             for k in range(TILES):
                 c = b * NQ + s * TILES + k
-                if f == 0:
+                if f == 0 or f in GMASK:
                     nc.tensor.matmul(out=pmk[:, k * P:(k + 1) * P], lhsT=ident_b[:, c:c + 1].to_broadcast([P, P]),
                                      rhs=pr[:], start=True, stop=True)
                 else:
@@ -158,8 +168,20 @@ def tile_attentivestatspool_pa_t_kernel(tc, x, mask, w1, b1, g1, be1, out):
         def mask_mul(f):
             b, s = divmod(f, NCH)
             xm = xmp.tile([P, PACK, CHUNK], BF16, name="xm")
-            nc.vector.tensor_tensor(out=xm[:], in0=raw[b][:, :, s * CHUNK:(s + 1) * CHUNK],
-                                    in1=mk.pop(f)[:].unsqueeze(1).to_broadcast([P, PACK, CHUNK]), op=ALU.mult)
+            for j in range(0, PACK, 2 if f == 0 else PACK):
+                n = 2 if f == 0 else PACK
+                nc.vector.tensor_tensor(out=xm[:, j:j + n, :], in0=raw[b][:, j:j + n, s * CHUNK:(s + 1) * CHUNK],
+                                        in1=mk[f][:].unsqueeze(1).to_broadcast([P, n, CHUNK]), op=ALU.mult)
+            xms[f] = xm
+
+        def mask_gp(f):
+            b, s = divmod(f, NCH)
+            mask_bc(f)
+            mkb = xmg.tile([P, CHUNK], BF16, name="mkb")
+            nc.scalar.copy(out=mkb[:], in_=mk[f][:])
+            xm = xmg.tile([P, PACK, CHUNK], BF16, name="xmg")
+            nc.gpsimd.tensor_tensor(out=xm[:], in0=raw[b][:, :, s * CHUNK:(s + 1) * CHUNK],
+                                    in1=mkb[:].unsqueeze(1).to_broadcast([P, PACK, CHUNK]), op=ALU.mult)
             xms[f] = xm
 
         def bn(f, j):
@@ -265,12 +287,14 @@ def tile_attentivestatspool_pa_t_kernel(tc, x, mask, w1, b1, g1, be1, out):
                 pss[g].append(ps)
 
         def p1(g):
-            a = up.tile([P, TILES, H], F32, name="a")
             for pair in range(TILES // 2):
-                nc.vector.tensor_tensor(out=a[:, 2 * pair:2 * pair + 2, :], in0=pss[g][pair][:],
-                                        in1=b1bc[:].unsqueeze(1).to_broadcast([P, 2, H]), op=ALU.add)
-            pss.pop(g)
-            av[g] = a
+                p1_half(g, pair)
+
+        def p1_half(g, pair):
+            if pair == 0:
+                av[g] = up.tile([P, TILES, H], F32, name="a")
+            nc.vector.tensor_tensor(out=av[g][:, 2 * pair:2 * pair + 2, :], in0=pss[g][pair][:],
+                                    in1=b1bc[:].unsqueeze(1).to_broadcast([P, 2, H]), op=ALU.add)
 
         def relu_square(g):
             a = av[g]
@@ -317,13 +341,15 @@ def tile_attentivestatspool_pa_t_kernel(tc, x, mask, w1, b1, g1, be1, out):
             nrm[g] = [(mv4[:, k, 0:1], rstd[:, k:k + 1]) for k in range(TILES)]
 
         def normalise(g, eng):
-            a = av.pop(g)
-            zh = zp.tile([P, TILES, H], F32, name="zh")
             for k in range(TILES):
-                mean, rstd = nrm[g][k]
-                eng.tensor_scalar(out=zh[:, k, :], in0=a[:, k, :], scalar1=mean, scalar2=rstd,
-                                  op0=ALU.subtract if g in VROUTE else ALU.add, op1=ALU.mult)
-            zhs[g] = zh
+                norm_piece(g, eng, k)
+
+        def norm_piece(g, eng, k):
+            if k == 0:
+                zhs[g] = zp.tile([P, TILES, H], F32, name="zh")
+            mean, rstd = nrm[g][k]
+            eng.tensor_scalar(out=zhs[g][:, k, :], in0=av[g][:, k, :], scalar1=mean, scalar2=rstd,
+                              op0=ALU.subtract if g in VROUTE else ALU.add, op1=ALU.mult)
 
         def p4(g):
             zh = zhs.pop(g)
@@ -365,34 +391,36 @@ def tile_attentivestatspool_pa_t_kernel(tc, x, mask, w1, b1, g1, be1, out):
 
         mask_bc(0)
         mask_mul(0)
+        for f in GMASK:
+            mask_gp(f)
         columns()
         mask_bc(1)
         regroup_to(RGA)
         for f in range(NG):
             i = f - LEAD
             b, s = divmod(f, NCH)
-            slots = [[], [], [], [], []]
+            slots = [[], [], [], [], [], []]
             if s == NCH - 1:
                 slots[1].append(lambda b=b: aggr(b, 0))
-                slots[2].append(lambda b=b: aggr(b, 1))
-                slots[3].append(lambda b=b: aggr(b, 2))
+                slots[3].append(lambda b=b: aggr(b, 1))
+                slots[4].append(lambda b=b: aggr(b, 2))
             if s == 0 and b > 0:
                 slots[0].append(lambda b=b: aggr(b - 1, 3))
                 ops = {}
                 for n in range(5):
-                    slots[n].append(lambda b=b, n=n: ops.setdefault("l", stat_ops(b - 1) if n == 0 else None)[n]())
-                slots[0], slots[1] = slots[0][:1], slots[0][1:] + slots[1]
+                    slots[n + 1].append(lambda b=b, n=n: ops.setdefault("l", stat_ops(b - 1) if n == 0 else None)[n]())
             if s == 1 and b > 0:
-                slots[1].append(lambda b=b: spread_q(b - 1, 0))
+                slots[0].append(lambda b=b: spread_q(b - 1, 0))
                 slots[2].append(lambda b=b: (spread_q(b - 1, 1), mx(NCH * (b - 1))))
             if f == 1:
                 ptot = totals_mm()
-                slots[2].append(lambda: totals(ptot))
+                slots[3].append(lambda: totals(ptot))
             if f == 3:
-                slots[3].append(w1_quant)
+                slots[4].append(w1_quant)
             if ok(i - 2):
                 norm_g(i - 2)
-                normalise(i - 2, nc.gpsimd)
+                if i - 2 < NG - 2 * NCH:
+                    normalise(i - 2, nc.gpsimd)
             if ok(i - 1):
                 relu_square(i - 1)
             if f == 1:
@@ -407,76 +435,89 @@ def tile_attentivestatspool_pa_t_kernel(tc, x, mask, w1, b1, g1, be1, out):
             regroup_to(f + 1 + RGA)
             for j in range(PACK):
                 bn(f, j)
-                if j == 1 and f + 1 < NG:
-                    mask_mul(f + 1)
-                    if f + 2 < NG:
-                        mask_bc(f + 2)
-                for fn in slots[j]:
+                for fn in slots[j if j < 2 else j + 1]:
                     fn()
-            for fn in slots[4]:
-                fn()
+                if j == 1:
+                    if f + 1 < NG and f + 1 not in GMASK:
+                        mask_mul(f + 1)
+                    if f + 2 < NG and f + 2 not in GMASK:
+                        mask_bc(f + 2)
+                    for fn in slots[2]:
+                        fn()
             if f >= 3:
                 quant_to(f + 1 if f < NG - 4 else NG - 4)
-            if ok(i):
+            for fn in slots[5]:
+                fn()
+            if f == NG - 1:
+                p1_half(i, 0)
+                aggr(b, 3)
+                p1_half(i, 1)
+            elif ok(i):
                 p1(i)
             if ok(i) and (i + 1) % NCH:
                 mx(i + 1)
         b = B - 1
         last = NG - NCH
-        aggr(b, 3)
-        ops = stat_ops(b)
-        quant_to(last + 1)
-        ops[0]()
         norm_g(last - 3)
-        quant_to(last + 2)
+        relu_square(last - 2)
+        ops = stat_ops(b)
+        ops[0]()
+        norm_piece(last - 4, nc.vector, 0)
+        norm_piece(last - 4, nc.vector, 1)
         ops[1]()
         spread(b, 0, fin[b]["m0"])
         ops[2]()
-        spread_q(b, 0)
+        norm_piece(last - 4, nc.vector, 2)
+        norm_piece(last - 4, nc.vector, 3)
         ops[3]()
-        quant_to(last + 3)
+        spread_q(b, 0)
         ops[4]()
-        relu_square(last - 2)
         p4(last - 4)
         tanh_store(last - 4)
-        normalise(last - 3, nc.vector)
+        quant_to(last + 1)
         p1(last - 1)
-        spread(b, 1, fin[b]["std"])
-        quant_to(last + 4)
-        spread_q(b, 1)
-        p4(last - 3)
-        mx(last)
         norm_g(last - 2)
         relu_square(last - 1)
-        tanh_store(last - 3)
-        normalise(last - 2, nc.vector)
+        spread(b, 1, fin[b]["std"])
+        norm_piece(last - 3, nc.vector, 0)
+        norm_piece(last - 3, nc.vector, 1)
+        spread_q(b, 1)
+        mx(last)
+        norm_piece(last - 3, nc.vector, 2)
+        norm_piece(last - 3, nc.vector, 3)
+        quant_to(last + 2)
         p1(last)
         mx(last + 1)
+        quant_to(last + 3)
         p1(last + 1)
         mx(last + 2)
+        p4(last - 3)
         relu_square(last)
-        norm_g(last - 1)
+        tanh_store(last - 3)
+        normalise(last - 2, nc.vector)
+        p1(last + 2)
+        quant_to(last + 4)
         p4(last - 2)
-        tanh_store(last - 2)
+        mx(last + 3)
+        relu_square(last + 2)
+        norm_g(last - 1)
         vroute(last + 1)
+        tanh_store(last - 2)
+        norm_g(last)
         norm_v(last + 1)
         normalise(last - 1, nc.vector)
-        norm_g(last)
-        p1(last + 2)
         p4(last - 1)
-        mx(last + 3)
+        p1(last + 3)
         tanh_store(last - 1)
         normalise(last, nc.vector)
-        normalise(last + 1, nc.vector)
         p4(last)
-        relu_square(last + 2)
-        tanh_store(last)
-        p1(last + 3)
-        p4(last + 1)
         vroute(last + 3)
+        tanh_store(last)
+        normalise(last + 1, nc.vector)
+        p4(last + 1)
+        tanh_store(last + 1)
         norm_g(last + 2)
         norm_v(last + 3)
-        tanh_store(last + 1)
         normalise(last + 2, nc.vector)
         p4(last + 2)
         tanh_store(last + 2)

@@ -24,9 +24,10 @@ EPS_LN = 1e-5
 EPS_STD = 1e-5
 LEAD = 5
 RGA = 3
-GMASK = [3, 5]
+GMASK = [3, 5, 7]
+VRG = []
 VNORM_FROM = 10
-VROUTE = [13, 15]
+VROUTE = [14]
 FLOPS = 2 * B * H * 3 * C * T
 
 
@@ -80,7 +81,7 @@ def tile_attentivestatspool_pa_t_kernel(tc, x, mask, w1, b1, g1, be1, out):
         nc.vector.memset(warm[:], 0.0)
         nc.scalar.activation(out=warm[:], in_=warm[:], func=ACT.Tanh)
         ones_t = const.tile([P, P], BF16, name="ones_t")
-        nc.vector.memset(ones_t[:], 1.0 / T)
+        nc.vector.memset(ones_t[:], 1.0)
         half = const.tile([P, PACK], F32, name="half")
         nc.vector.memset(half[:], 0.5)
         nhalf = const.tile([P, TILES], F32, name="nhalf")
@@ -90,25 +91,28 @@ def tile_attentivestatspool_pa_t_kernel(tc, x, mask, w1, b1, g1, be1, out):
         w1s = const.tile([P, 3, H], U8, name="w1s", align_bytes=64)
         w1g = const.tile([P, 3, H, PACK], BF16, name="w1g", align_bytes=64)
         cols = const.tile([P, B * NQ], BF16, name="cols")
+        cols1 = const.tile([P, B * NQ], BF16, name="cols1")
         gb = const.tile([P, 4], F32, name="gb")
         b1c = const.tile([P, 2], BF16, name="b1c")
-        r_t = const.tile([P, B], F32, name="r_t")
+        st = const.tile([P, B, PACK, NCH * 6 + 3], F32, name="st")
+        nc.gpsimd.memset(st[:], 0.0)
         b1bc = const.tile([P, H], BF16, name="b1bc")
 
         def columns():
             ps_pr = ps_ms.tile([P, P], BF16, tag="ms", name="ps_pr")
             nc.tensor.transpose(out=ps_pr[:], in_=pr[:], identity=ident_b[:])
             nc.vector.tensor_copy(out=cols[:], in_=ps_pr[:, 0:B * NQ])
+            nc.vector.tensor_scalar(out=cols1[:], in0=ps_pr[:, 0:B * NQ], scalar1=-1.0, scalar2=None, op0=ALU.add)
 
         def totals_mm():
             ps_tot = ps_ms.tile([P, B * NQ], F32, tag="ms", name="ps_tot")
-            nc.tensor.matmul(out=ps_tot[:], lhsT=ones_t[:], rhs=cols[:], start=True, stop=True)
+            nc.tensor.matmul(out=ps_tot[:], lhsT=ones_t[:], rhs=cols1[:], start=True, stop=True)
             return ps_tot
 
         def totals(ps_tot):
-            tot = const.tile([P, B], F32, name="tot")
-            nc.vector.tensor_reduce(out=tot[:], in_=ps_tot[:].rearrange("p (b q) -> p b q", b=B), axis=AX.X, op=ALU.add)
-            nc.vector.reciprocal(out=r_t[:], in_=tot[:])
+            nc.vector.tensor_reduce(out=st[:, :, :, NCH * 6], axis=AX.X, op=ALU.add,
+                                    in_=ps_tot[:].rearrange("p (b q) -> p b q", b=B).unsqueeze(2)
+                                    .to_broadcast([P, B, PACK, NQ]))
 
         def params():
             ps_par = ps_ms.tile([P, P], BF16, tag="ms", name="ps_par")
@@ -141,8 +145,7 @@ def tile_attentivestatspool_pa_t_kernel(tc, x, mask, w1, b1, g1, be1, out):
 
         xc = {}
         xs = {}
-        st = {}
-        rows = {}
+        vb = {}
         gr = {}
         mk = {}
         fin = {}
@@ -155,7 +158,7 @@ def tile_attentivestatspool_pa_t_kernel(tc, x, mask, w1, b1, g1, be1, out):
                 pmk = ps_mk.tile([P, CHUNK], BF16, name="pmk")
             for k in range(TILES):
                 c = b * NQ + s * TILES + k
-                if f == 0 or f in GMASK:
+                if f == 0 or f in GMASK[0:2]:
                     nc.tensor.matmul(out=pmk[:, k * P:(k + 1) * P], lhsT=ident_b[:, c:c + 1].to_broadcast([P, P]),
                                      rhs=pr[:], start=True, stop=True)
                 else:
@@ -174,11 +177,10 @@ def tile_attentivestatspool_pa_t_kernel(tc, x, mask, w1, b1, g1, be1, out):
                                         in1=mk[f][:].unsqueeze(1).to_broadcast([P, n, CHUNK]), op=ALU.mult)
             xms[f] = xm
 
-        def mask_gp(f):
+        def mask_gp(f, copy):
             b, s = divmod(f, NCH)
-            mask_bc(f)
             mkb = xmg.tile([P, CHUNK], BF16, name="mkb")
-            nc.scalar.copy(out=mkb[:], in_=mk[f][:])
+            copy(out=mkb[:], in_=mk[f][:])
             xm = xmg.tile([P, PACK, CHUNK], BF16, name="xmg")
             nc.gpsimd.tensor_tensor(out=xm[:], in0=raw[b][:, :, s * CHUNK:(s + 1) * CHUNK],
                                     in1=mkb[:].unsqueeze(1).to_broadcast([P, PACK, CHUNK]), op=ALU.mult)
@@ -186,9 +188,7 @@ def tile_attentivestatspool_pa_t_kernel(tc, x, mask, w1, b1, g1, be1, out):
 
         def bn(f, j):
             b, s = divmod(f, NCH)
-            if s == 0 and j == 0:
-                st[b] = per.tile([P, PACK, NCH, 6], F32, name="st")
-            nc.vector.bn_stats(out=st[b][:, j, s, :], in_=xms[f][:, j, :])
+            nc.vector.bn_stats(out=st[:, b, j, s * 6:(s + 1) * 6], in_=xms[f][:, j, :])
 
         def regroup(f):
             b, s = divmod(f, NCH)
@@ -196,6 +196,14 @@ def tile_attentivestatspool_pa_t_kernel(tc, x, mask, w1, b1, g1, be1, out):
             grouped = grp.tile([P, CHUNK, PACK], BF16, name="grouped", align_bytes=64)
             nc.scalar.copy(out=grouped[:].rearrange("p (c i) j -> p c j i", i=4),
                            in_=raw[b][:, :, cols_f].rearrange("p j (c i) -> p c j i", i=4))
+            gr[f] = grouped
+
+        def regroup_v(f):
+            b, s = divmod(f, NCH)
+            cols_f = slice(s * CHUNK, (s + 1) * CHUNK)
+            grouped = grp.tile([P, CHUNK, PACK], BF16, name="grouped", align_bytes=64)
+            nc.vector.tensor_copy(out=grouped[:].rearrange("p (c i) j -> p c j i", i=4),
+                                  in_=raw[b][:, :, cols_f].rearrange("p j (c i) -> p c j i", i=4))
             gr[f] = grouped
 
         def quant(f):
@@ -210,64 +218,42 @@ def tile_attentivestatspool_pa_t_kernel(tc, x, mask, w1, b1, g1, be1, out):
         def aggr(b, j):
             if j == 0:
                 fin[b] = {"mv": per.tile([P, PACK, 2], F32, name="mv")}
-            nc.vector.bn_aggr(out=fin[b]["mv"][:, j, :], in_=st[b][:, j].rearrange("p s k -> p (s k)"))
+            nc.vector.bn_aggr(out=fin[b]["mv"][:, j, :], in_=st[:, b, j, :])
 
-        def stat_ops(b):
-            e = fin[b]
-            mean = e["mv"][:, :, 0]
-            var = e["mv"][:, :, 1]
-            rb = r_t[:, b:b + 1]
-            m0 = per.tile([P, PACK], F32, name="m0")
-            d = per.tile([P, PACK], F32, name="d")
+        def std_of(b, eng):
+            mv = fin[b]["mv"]
             v0 = per.tile([P, PACK], F32, name="v0")
-            e["m0"] = m0
-            e["v0"] = v0
-            on_g = b < B - 1
+            eng.tensor_scalar(out=v0[:], in0=mv[:, :, 1], scalar1=EPS_STD, scalar2=0.0, op0=ALU.max, op1=ALU.add)
+            nc.gpsimd.tensor_tensor(out=mv[:, :, 1], in0=v0[:], in1=half[:], op=ALU.pow)
 
-            def first():
-                nc.vector.tensor_scalar(out=m0[:], in0=mean, scalar1=rb, scalar2=None, op0=ALU.mult)
-                if on_g:
-                    spread(b, 0, m0)
-
-            def last():
-                nc.vector.tensor_scalar(out=v0[:], in0=v0[:], scalar1=EPS_STD, scalar2=None, op0=ALU.max)
-                std = per.tile([P, PACK], F32, name="std")
-                nc.gpsimd.tensor_tensor(out=std[:], in0=v0[:], in1=half[:], op=ALU.pow)
-                e["std"] = std
-                if on_g:
-                    spread(b, 1, std)
-
-            return [
-                first,
-                lambda: nc.vector.tensor_tensor(out=d[:], in0=mean, in1=m0[:], op=ALU.subtract),
-                lambda: nc.vector.tensor_tensor(out=d[:], in0=m0[:], in1=d[:], op=ALU.mult),
-                lambda: nc.vector.scalar_tensor_tensor(out=v0[:], in0=var, scalar=rb, in1=d[:],
-                                                       op0=ALU.mult, op1=ALU.add),
-                last,
-            ]
-
-        def spread(b, gi, src):
+        def spread(b):
             e = fin[b]
-            msb = per.tile([P, P, PACK], BF16, name="msb%d" % gi, align_bytes=64)
-            if b < B - 1:
-                nc.gpsimd.tensor_scalar(out=msb[:], in0=src[:].unsqueeze(1).to_broadcast([P, P, PACK]),
-                                        scalar1=1.0, scalar2=0.0, op0=ALU.mult, op1=ALU.add)
-            else:
-                nc.vector.tensor_copy(out=msb[:], in_=src[:].unsqueeze(1).to_broadcast([P, P, PACK]))
-            e["msb%d" % gi] = msb
+            e["msb"] = per.tile([P, 2, P, PACK], BF16, name="msb", align_bytes=64)
+            nc.vector.tensor_copy(out=e["msb"][:], in_=e["mv"][:].rearrange("p j k -> p k j").unsqueeze(2)
+                                  .to_broadcast([P, 2, P, PACK]))
 
-        def spread_q(b, gi):
+        def spread_q(b):
             e = fin[b]
-            msb = e["msb%d" % gi]
-            mc = per.tile([P, P], U32, name="mc%d" % gi, align_bytes=64)
-            msc = per.tile([P, P], U8, name="msc%d" % gi, align_bytes=64)
-            nc.vector.quantize_mx(out=mc[:].bitcast(FP8X4), scales=msc[:], in_=msb[:].rearrange("p w j -> p (w j)"))
-            rows[(b, gi)] = (mc, msc)
+            mc = per.tile([P, 2 * P], U32, name="mc", align_bytes=64)
+            msc = per.tile([P, 2 * P], U8, name="msc", align_bytes=64)
+            nc.vector.quantize_mx(out=mc[:].bitcast(FP8X4), scales=msc[:],
+                                  in_=e["msb"][:].rearrange("p k w j -> p (k w j)"))
+            e["ps"] = ps_ms.tile([P, H], F32, tag="ms", name="ps_vb")
+            for gi in range(2):
+                nc.tensor.matmul_mx(out=e["ps"][:], lhsT=mc[:, gi * P:(gi + 1) * P].bitcast(FP8X4),
+                                    lhsT_scale=msc[:, gi * P:(gi + 1) * P],
+                                    rhs=w1c[:, 1 + gi, :].bitcast(FP8X4), rhs_scale=w1s[:, 1 + gi, :],
+                                    start=(gi == 0), stop=(gi == 1))
+
+        def bias_row(b):
+            vb[b] = per.tile([P, H], F32, name="vb")
+            nc.vector.tensor_tensor(out=vb[b][:], in0=fin.pop(b)["ps"][:], in1=b1bc[:], op=ALU.add)
 
         pss = {}
         av = {}
         ln = {}
         nrm = {}
+        ves = {}
         zhs = {}
         pts = {}
 
@@ -278,12 +264,10 @@ def tile_attentivestatspool_pa_t_kernel(tc, x, mask, w1, b1, g1, be1, out):
                 ps = ps_mx.tile([P, 2, H], F32, name="ps")
                 for i in range(2):
                     t0 = s * CHUNK + (2 * pair + i) * P
-                    stat = [(xc[b][:, t0:t0 + P], xs[b][:, t0:t0 + P])]
-                    stat += [(rows[(b, gi)][0][:], rows[(b, gi)][1][:]) for gi in range(2)]
-                    for n in range(3):
-                        nc.tensor.matmul_mx(out=ps[:, i, :], lhsT=stat[n][0].bitcast(FP8X4), lhsT_scale=stat[n][1],
-                                            rhs=w1c[:, n, :].bitcast(FP8X4), rhs_scale=w1s[:, n, :],
-                                            start=(n == 0), stop=(n == 2))
+                    nc.tensor.matmul_mx(out=ps[:, i, :], lhsT=xc[b][:, t0:t0 + P].bitcast(FP8X4),
+                                        lhsT_scale=xs[b][:, t0:t0 + P],
+                                        rhs=w1c[:, 0, :].bitcast(FP8X4), rhs_scale=w1s[:, 0, :],
+                                        start=True, stop=True)
                 pss[g].append(ps)
 
         def p1(g):
@@ -294,7 +278,7 @@ def tile_attentivestatspool_pa_t_kernel(tc, x, mask, w1, b1, g1, be1, out):
             if pair == 0:
                 av[g] = up.tile([P, TILES, H], F32, name="a")
             nc.vector.tensor_tensor(out=av[g][:, 2 * pair:2 * pair + 2, :], in0=pss[g][pair][:],
-                                    in1=b1bc[:].unsqueeze(1).to_broadcast([P, 2, H]), op=ALU.add)
+                                    in1=vb[g // NCH][:].unsqueeze(1).to_broadcast([P, 2, H]), op=ALU.add)
 
         def relu_square(g):
             a = av[g]
@@ -309,20 +293,32 @@ def tile_attentivestatspool_pa_t_kernel(tc, x, mask, w1, b1, g1, be1, out):
                                      bias=mu[:, k:k + 1], accum_out=sq[:, k:k + 1])
             ln[g] = (mu, sq)
 
-        def norm_g(g):
-            mu, sq = ln.pop(g)
-            negmu = sml.tile([P, TILES], F32, name="negmu")
-            nc.gpsimd.tensor_scalar(out=negmu[:], in0=mu[:], scalar1=-1.0 / H, scalar2=0.0, op0=ALU.mult, op1=ALU.add)
+        def var_v(g):
             ve = sml.tile([P, TILES], F32, name="ve")
-            nc.gpsimd.tensor_scalar(out=ve[:], in0=sq[:], scalar1=1.0 / H**3, scalar2=EPS_LN / H**2,
-                                    op0=ALU.mult, op1=ALU.add)
-            rstd = sml.tile([P, TILES], F32, name="rstd")
-            nc.gpsimd.tensor_tensor(out=rstd[:], in0=ve[:], in1=nhalf[:], op=ALU.pow)
-            nrm[g] = [(negmu[:, k:k + 1], rstd[:, k:k + 1]) for k in range(TILES)]
+            if g in VROUTE:
+                nc.vector.tensor_scalar(out=ve[:], in0=ln[g][:, :, 1], scalar1=1.0, scalar2=EPS_LN,
+                                        op0=ALU.mult, op1=ALU.add)
+            else:
+                nc.vector.tensor_scalar(out=ve[:], in0=ln[g][1][:], scalar1=1.0 / H**3, scalar2=EPS_LN / H**2,
+                                        op0=ALU.mult, op1=ALU.add)
+            ves[g] = ve
 
-        def vroute(g):
+        def rstd_g(g):
+            rstd = sml.tile([P, TILES], F32, name="rstd")
+            nc.gpsimd.tensor_tensor(out=rstd[:], in0=ves.pop(g)[:], in1=nhalf[:], op=ALU.pow)
+            if g in VROUTE:
+                nrm[g] = [(ln[g][:, k, 0:1], rstd[:, k:k + 1]) for k in range(TILES)]
+            else:
+                negmu = sml.tile([P, TILES], F32, name="negmu")
+                nc.gpsimd.tensor_scalar(out=negmu[:], in0=ln[g][0][:], scalar1=-1.0 / H, scalar2=0.0,
+                                        op0=ALU.mult, op1=ALU.add)
+                nrm[g] = [(negmu[:, k:k + 1], rstd[:, k:k + 1]) for k in range(TILES)]
+
+        def relu_v(g):
+            nc.vector.tensor_scalar(out=av[g][:], in0=av[g][:], scalar1=0.0, scalar2=None, op0=ALU.max)
+
+        def stats_v(g):
             a = av[g]
-            nc.vector.tensor_scalar(out=a[:], in0=a[:], scalar1=0.0, scalar2=None, op0=ALU.max)
             st4 = sml.tile([P, TILES, 6], F32, name="st4")
             mv4 = sml.tile([P, TILES, 2], F32, name="mv4")
             for k in range(TILES):
@@ -330,15 +326,6 @@ def tile_attentivestatspool_pa_t_kernel(tc, x, mask, w1, b1, g1, be1, out):
             for k in range(TILES):
                 nc.vector.bn_aggr(out=mv4[:, k, :], in_=st4[:, k, :])
             ln[g] = mv4
-
-        def norm_v(g):
-            mv4 = ln.pop(g)
-            ve = sml.tile([P, TILES], F32, name="ve")
-            nc.gpsimd.tensor_scalar(out=ve[:], in0=mv4[:, :, 1], scalar1=1.0, scalar2=EPS_LN,
-                                    op0=ALU.mult, op1=ALU.add)
-            rstd = sml.tile([P, TILES], F32, name="rstd")
-            nc.gpsimd.tensor_tensor(out=rstd[:], in0=ve[:], in1=nhalf[:], op=ALU.pow)
-            nrm[g] = [(mv4[:, k, 0:1], rstd[:, k:k + 1]) for k in range(TILES)]
 
         def normalise(g, eng):
             for k in range(TILES):
@@ -381,7 +368,10 @@ def tile_attentivestatspool_pa_t_kernel(tc, x, mask, w1, b1, g1, be1, out):
 
         def regroup_to(n):
             while done["rg"] < min(NG, n):
-                regroup(done["rg"])
+                if done["rg"] in VRG:
+                    regroup_v(done["rg"])
+                else:
+                    regroup(done["rg"])
                 done["rg"] = done["rg"] + 1
 
         def quant_to(n):
@@ -391,36 +381,33 @@ def tile_attentivestatspool_pa_t_kernel(tc, x, mask, w1, b1, g1, be1, out):
 
         mask_bc(0)
         mask_mul(0)
-        for f in GMASK:
-            mask_gp(f)
+        for f in GMASK[0:2]:
+            mask_bc(f)
+        regroup_to(1)
+        for f in GMASK[0:2]:
+            mask_gp(f, nc.scalar.copy)
         columns()
         mask_bc(1)
         regroup_to(RGA)
         for f in range(NG):
             i = f - LEAD
             b, s = divmod(f, NCH)
-            slots = [[], [], [], [], [], []]
-            if s == NCH - 1:
-                slots[1].append(lambda b=b: aggr(b, 0))
-                slots[3].append(lambda b=b: aggr(b, 1))
-                slots[4].append(lambda b=b: aggr(b, 2))
-            if s == 0 and b > 0:
-                slots[0].append(lambda b=b: aggr(b - 1, 3))
-                ops = {}
-                for n in range(5):
-                    slots[n + 1].append(lambda b=b, n=n: ops.setdefault("l", stat_ops(b - 1) if n == 0 else None)[n]())
+            if f == 4:
+                w1_quant()
+            if f >= 4:
+                quant_to(min(f, NG - NCH))
             if s == 1 and b > 0:
-                slots[0].append(lambda b=b: spread_q(b - 1, 0))
-                slots[2].append(lambda b=b: (spread_q(b - 1, 1), mx(NCH * (b - 1))))
+                spread(b - 1)
+                spread_q(b - 1)
+            if f + 2 in GMASK[2:]:
+                mask_gp(f + 2, nc.vector.tensor_copy)
+            if ok(i - 2):
+                var_v(i - 2)
+                rstd_g(i - 2)
             if f == 1:
                 ptot = totals_mm()
-                slots[3].append(lambda: totals(ptot))
-            if f == 3:
-                slots[4].append(w1_quant)
-            if ok(i - 2):
-                norm_g(i - 2)
-                if i - 2 < NG - 2 * NCH:
-                    normalise(i - 2, nc.gpsimd)
+            if ok(i - 3):
+                p4(i - 3)
             if ok(i - 1):
                 relu_square(i - 1)
             if f == 1:
@@ -430,94 +417,94 @@ def tile_attentivestatspool_pa_t_kernel(tc, x, mask, w1, b1, g1, be1, out):
             if f == 3:
                 params_b1()
             if ok(i - 3):
-                p4(i - 3)
                 tanh_store(i - 3)
             regroup_to(f + 1 + RGA)
             for j in range(PACK):
                 bn(f, j)
-                for fn in slots[j if j < 2 else j + 1]:
-                    fn()
+                if j == 0 and s == 0 and b > 0:
+                    aggr(b - 1, 3)
+                    std_of(b - 1, nc.gpsimd)
+                if j == 0 and 0 <= i - 2 < NG - 2 * NCH:
+                    normalise(i - 2, nc.gpsimd)
+                if j > 0 and s == NCH - 1:
+                    aggr(b, j - 1)
                 if j == 1:
                     if f + 1 < NG and f + 1 not in GMASK:
                         mask_mul(f + 1)
                     if f + 2 < NG and f + 2 not in GMASK:
                         mask_bc(f + 2)
-                    for fn in slots[2]:
-                        fn()
-            if f >= 3:
-                quant_to(f + 1 if f < NG - 4 else NG - 4)
-            for fn in slots[5]:
-                fn()
-            if f == NG - 1:
-                p1_half(i, 0)
-                aggr(b, 3)
-                p1_half(i, 1)
-            elif ok(i):
+                    if f + 3 in GMASK[2:]:
+                        mask_bc(f + 3)
+                if j == 2 and f == 1:
+                    totals(ptot)
+                if j == 2 and s == 1 and b > 0:
+                    bias_row(b - 1)
+            if i == -1:
+                mx(0)
+            if ok(i) and f < NG - 1:
                 p1(i)
-            if ok(i) and (i + 1) % NCH:
                 mx(i + 1)
         b = B - 1
         last = NG - NCH
-        norm_g(last - 3)
+        p1_half(last - 2, 0)
+        aggr(b, 3)
+        std_of(b, nc.vector)
+        p1_half(last - 2, 1)
+        mx(last - 1)
         relu_square(last - 2)
-        ops = stat_ops(b)
-        ops[0]()
-        norm_piece(last - 4, nc.vector, 0)
-        norm_piece(last - 4, nc.vector, 1)
-        ops[1]()
-        spread(b, 0, fin[b]["m0"])
-        ops[2]()
-        norm_piece(last - 4, nc.vector, 2)
-        norm_piece(last - 4, nc.vector, 3)
-        ops[3]()
-        spread_q(b, 0)
-        ops[4]()
-        p4(last - 4)
-        tanh_store(last - 4)
-        quant_to(last + 1)
         p1(last - 1)
-        norm_g(last - 2)
-        relu_square(last - 1)
-        spread(b, 1, fin[b]["std"])
-        norm_piece(last - 3, nc.vector, 0)
-        norm_piece(last - 3, nc.vector, 1)
-        spread_q(b, 1)
+        spread(b)
+        spread_q(b)
+        quant_to(last + 1)
         mx(last)
-        norm_piece(last - 3, nc.vector, 2)
-        norm_piece(last - 3, nc.vector, 3)
-        quant_to(last + 2)
+        normalise(last - 4, nc.vector)
+        p4(last - 4)
+        bias_row(b)
+        var_v(last - 3)
+        rstd_g(last - 3)
+        relu_square(last - 1)
+        tanh_store(last - 4)
         p1(last)
-        mx(last + 1)
+        relu_square(last)
         quant_to(last + 3)
+        mx(last + 1)
+        normalise(last - 3, nc.vector)
+        p4(last - 3)
+        var_v(last - 2)
+        var_v(last - 1)
+        rstd_g(last - 2)
+        rstd_g(last - 1)
         p1(last + 1)
         mx(last + 2)
-        p4(last - 3)
-        relu_square(last)
-        tanh_store(last - 3)
-        normalise(last - 2, nc.vector)
         p1(last + 2)
         quant_to(last + 4)
-        p4(last - 2)
         mx(last + 3)
-        relu_square(last + 2)
-        norm_g(last - 1)
-        vroute(last + 1)
+        relu_square(last + 1)
+        tanh_store(last - 3)
+        relu_v(last + 2)
+        normalise(last - 2, nc.vector)
+        p4(last - 2)
         tanh_store(last - 2)
-        norm_g(last)
-        norm_v(last + 1)
         normalise(last - 1, nc.vector)
         p4(last - 1)
+        var_v(last)
+        var_v(last + 1)
+        rstd_g(last)
+        rstd_g(last + 1)
         p1(last + 3)
+        relu_square(last + 3)
+        stats_v(last + 2)
         tanh_store(last - 1)
         normalise(last, nc.vector)
         p4(last)
-        vroute(last + 3)
         tanh_store(last)
         normalise(last + 1, nc.vector)
         p4(last + 1)
         tanh_store(last + 1)
-        norm_g(last + 2)
-        norm_v(last + 3)
+        var_v(last + 2)
+        var_v(last + 3)
+        rstd_g(last + 2)
+        rstd_g(last + 3)
         normalise(last + 2, nc.vector)
         p4(last + 2)
         tanh_store(last + 2)

@@ -24,10 +24,16 @@ EPS_LN = 1e-5
 EPS_STD = 1e-5
 LEAD = 5
 RGA = 3
-GMASK = [3, 5, 7]
-VRG = []
+RGB = 5
+SROW = []
+GM0 = [3, 4]
+GMASK = GM0 + [8]
+GC = [5, 6, 7]
+SNORM = [0]
+VEG = list(range(0, 16))
+GRG = [1, 8, 9]
 VNORM_FROM = 10
-VROUTE = [14]
+VROUTE = [12, 15]
 FLOPS = 2 * B * H * 3 * C * T
 
 
@@ -35,9 +41,10 @@ def tile_attentivestatspool_pa_t_kernel(tc, x, mask, w1, b1, g1, be1, out):
     nc = tc.nc
     with ExitStack() as ctx:
         const = ctx.enter_context(tc.tile_pool(name="const", bufs=1))
-        xmp = ctx.enter_context(tc.tile_pool(name="xmp", bufs=3))
-        xmg = ctx.enter_context(tc.tile_pool(name="xmg", bufs=2))
-        grp = ctx.enter_context(tc.tile_pool(name="grp", bufs=6))
+        rawp = ctx.enter_context(tc.tile_pool(name="rawp", bufs=10))
+        xmp = ctx.enter_context(tc.tile_pool(name="xmp", bufs=2))
+        xmg = ctx.enter_context(tc.tile_pool(name="xmg", bufs=3))
+        grp = ctx.enter_context(tc.tile_pool(name="grp", bufs=8))
         cod = ctx.enter_context(tc.tile_pool(name="cod", bufs=3))
         sml = ctx.enter_context(tc.tile_pool(name="sml", bufs=6))
         per = ctx.enter_context(tc.tile_pool(name="per", bufs=2))
@@ -50,28 +57,30 @@ def tile_attentivestatspool_pa_t_kernel(tc, x, mask, w1, b1, g1, be1, out):
         ps_mk = ctx.enter_context(tc.psum_pool(name="ps_mk", bufs=1))
         ctx.enter_context(tc.manual_schedule())
 
-        raw = [const.tile([P, PACK, T], BF16, name="raw%d" % b) for b in range(B)]
         w1_sb = const.tile([P, 2, 3 * C], BF16, name="w1_sb")
         pr = const.tile([P, P], BF16, name="pr")
         prm = const.tile([P, P], BF16, name="prm")
         x_v = [x[b].rearrange("(p j) t -> p j t", j=PACK) for b in range(B)]
+        raw = {}
+
+        def load(f):
+            b, s = divmod(f, NCH)
+            raw[f] = rawp.tile([P, PACK, CHUNK], BF16, name="rawc")
+            n = 2 if f == 0 else PACK
+            for j in range(0, PACK, n):
+                nc.sync.dma_start(out=raw[f][:, j:j + n, :], in_=x_v[b][:, j:j + n, s * CHUNK:(s + 1) * CHUNK])
+
         nc.scalar.dma_start(out=pr[0:B * NQ, :], in_=mask.rearrange("b o (q r) -> (b o q) r", r=P))
         nc.vector.memset(pr[B * NQ:P, :], 0.0)
         nc.vector.memset(prm[:], 0.0)
-        for j in (0, 2):
-            nc.sync.dma_start(out=raw[0][:, j:j + 2, 0:CHUNK], in_=x_v[0][:, j:j + 2, 0:CHUNK])
-        for s in range(1, NCH):
-            nc.sync.dma_start(out=raw[0][:, :, s * CHUNK:(s + 1) * CHUNK],
-                              in_=x_v[0][:, :, s * CHUNK:(s + 1) * CHUNK])
+        for f in range(6):
+            load(f)
         nc.sync.dma_start(out=w1_sb[:], in_=w1.rearrange("(hh p) k -> p hh k", p=P))
         nc.sync.dma_start(out=prm[0:2, :], in_=g1.rearrange("(r f) -> r f", f=P))
         nc.sync.dma_start(out=prm[2:4, :], in_=be1.rearrange("(r f) -> r f", f=P))
         nc.sync.dma_start(out=prm[4:6, :], in_=b1.rearrange("(r f) -> r f", f=P))
-        for b in range(1, B):
-            for s in range(0, NCH, NCH if b > 1 else 2):
-                n = NCH if b > 1 else 2
-                nc.sync.dma_start(out=raw[b][:, :, s * CHUNK:(s + n) * CHUNK],
-                                  in_=x_v[b][:, :, s * CHUNK:(s + n) * CHUNK])
+        for f in range(6, NG):
+            load(f)
 
         ident_b = const.tile([P, P], BF16, name="ident_b")
         make_identity(nc, ident_b[:])
@@ -95,7 +104,15 @@ def tile_attentivestatspool_pa_t_kernel(tc, x, mask, w1, b1, g1, be1, out):
         gb = const.tile([P, 4], F32, name="gb")
         b1c = const.tile([P, 2], BF16, name="b1c")
         st = const.tile([P, B, PACK, NCH * 6 + 3], F32, name="st")
-        nc.gpsimd.memset(st[:], 0.0)
+        nc.vector.memset(st[:], 0.0)
+        xmt = {}
+        for f in GC:
+            xmt[f] = const.tile([P, TILES, PACK, P + 2], BF16, name="xmt%d" % f)
+            nc.vector.memset(xmt[f][:, :, :, P:P + 2], 1.0)
+        for b in sorted(set(f // NCH for f in GC)):
+            fs = [f for f in GC if f // NCH == b]
+            s = fs[0] % NCH
+            nc.vector.memset(st[:, b, :, s * 6:s * 6 + 1], float(len(fs) * CHUNK))
         b1bc = const.tile([P, H], BF16, name="b1bc")
 
         def columns():
@@ -158,7 +175,7 @@ def tile_attentivestatspool_pa_t_kernel(tc, x, mask, w1, b1, g1, be1, out):
                 pmk = ps_mk.tile([P, CHUNK], BF16, name="pmk")
             for k in range(TILES):
                 c = b * NQ + s * TILES + k
-                if f == 0 or f in GMASK[0:2]:
+                if f == 0 or f in GM0:
                     nc.tensor.matmul(out=pmk[:, k * P:(k + 1) * P], lhsT=ident_b[:, c:c + 1].to_broadcast([P, P]),
                                      rhs=pr[:], start=True, stop=True)
                 else:
@@ -173,7 +190,7 @@ def tile_attentivestatspool_pa_t_kernel(tc, x, mask, w1, b1, g1, be1, out):
             xm = xmp.tile([P, PACK, CHUNK], BF16, name="xm")
             for j in range(0, PACK, 2 if f == 0 else PACK):
                 n = 2 if f == 0 else PACK
-                nc.vector.tensor_tensor(out=xm[:, j:j + n, :], in0=raw[b][:, j:j + n, s * CHUNK:(s + 1) * CHUNK],
+                nc.vector.tensor_tensor(out=xm[:, j:j + n, :], in0=raw[f][:, j:j + n, :],
                                         in1=mk[f][:].unsqueeze(1).to_broadcast([P, n, CHUNK]), op=ALU.mult)
             xms[f] = xm
 
@@ -182,7 +199,7 @@ def tile_attentivestatspool_pa_t_kernel(tc, x, mask, w1, b1, g1, be1, out):
             mkb = xmg.tile([P, CHUNK], BF16, name="mkb")
             copy(out=mkb[:], in_=mk[f][:])
             xm = xmg.tile([P, PACK, CHUNK], BF16, name="xmg")
-            nc.gpsimd.tensor_tensor(out=xm[:], in0=raw[b][:, :, s * CHUNK:(s + 1) * CHUNK],
+            nc.gpsimd.tensor_tensor(out=xm[:], in0=raw[f][:],
                                     in1=mkb[:].unsqueeze(1).to_broadcast([P, PACK, CHUNK]), op=ALU.mult)
             xms[f] = xm
 
@@ -190,20 +207,101 @@ def tile_attentivestatspool_pa_t_kernel(tc, x, mask, w1, b1, g1, be1, out):
             b, s = divmod(f, NCH)
             nc.vector.bn_stats(out=st[:, b, j, s * 6:(s + 1) * 6], in_=xms[f][:, j, :])
 
+        xts = {}
+        gps = {}
+
+        def turn(f, h):
+            xt = ps_tr.tile([P, 2, CHUNK], BF16, tag="tr", name="xt")
+            for n in range(2):
+                k = 2 * h + n
+                for j in range(PACK):
+                    nc.tensor.transpose(out=xt[:, n, j * P:(j + 1) * P], in_=raw[f][:, j, k * P:(k + 1) * P],
+                                        identity=ident_b[:])
+            xts[(f, h)] = xt
+
+        def turned_mask(f, h):
+            b, s = divmod(f, NCH)
+            xt = xts.pop((f, h))
+            for n in range(2):
+                k = 2 * h + n
+                c = b * NQ + s * TILES + k
+                nc.vector.tensor_scalar(out=xmt[f][:, k, :, 0:P], in0=xt[:, n, :].rearrange("p (j q) -> p j q", j=PACK),
+                                        scalar1=cols[:, c:c + 1], scalar2=None, op0=ALU.mult)
+
+        def gram(b, h):
+            pool, tag = (ps_ms, "ms") if h == 0 else (ps_tr, "tr")
+            gp = pool.tile([P, 2, P + 1], F32, tag=tag, name="gp")
+            fs = [f for f in GC if f // NCH == b]
+            for n in range(2):
+                j = 2 * h + n
+                for f in fs:
+                    for k in range(TILES):
+                        nc.tensor.matmul(out=gp[:, n, :], lhsT=xmt[f][:, k, j, 0:P], rhs=xmt[f][:, k, j, 0:P + 1],
+                                         start=(f == fs[0] and k == 0), stop=(f == fs[-1] and k == TILES - 1))
+            gps[(b, h)] = gp
+
+        def gram_triple(b, h):
+            gp = gps[(b, h)]
+            fs = [f for f in GC if f // NCH == b]
+            s = fs[0] % NCH
+            n_f = len(fs) * CHUNK
+            s2 = sml.tile([P, 2], F32, name="s2")
+            sm = sml.tile([P, 2], F32, name="smg")
+            mean = st[:, b, 2 * h:2 * h + 2, s * 6 + 1]
+
+            def diagonals():
+                for n in range(2):
+                    junk = zp.tile([P, P], F32, name="junkg")
+                    nc.vector.scalar_tensor_tensor(out=junk[:], in0=gp[:, n, 0:P], scalar=1.0, in1=ident_f[:],
+                                                   op0=ALU.mult, op1=ALU.mult, accum_out=s2[:, n:n + 1])
+                nc.vector.tensor_scalar(out=mean, in0=gp[:, :, P], scalar1=1.0 / n_f, scalar2=None, op0=ALU.mult)
+
+            return [
+                diagonals,
+                lambda: nc.vector.tensor_tensor(out=sm[:], in0=gp[:, :, P], in1=mean, op=ALU.mult),
+                lambda: nc.vector.tensor_tensor(out=st[:, b, 2 * h:2 * h + 2, s * 6 + 2], in0=s2[:], in1=sm[:],
+                                                op=ALU.subtract),
+            ]
+
+        srow = {}
+
+        def row_sums(f):
+            s12 = sml.tile([P, 2], F32, name="s12")
+            for n, func in enumerate((ACT.Identity, ACT.Square)):
+                junk = zp.tile([P, CHUNK], BF16, name="junkr")
+                nc.scalar.activation(out=junk[:], in_=xms[f][:, PACK - 1, :], func=func, accum_out=s12[:, n:n + 1])
+            srow[f] = s12
+
+        def row_triple(f):
+            b, s = divmod(f, NCH)
+            s12 = srow[f]
+            nc.gpsimd.tensor_scalar(out=st[:, b, PACK - 1, s * 6 + 1:s * 6 + 2], in0=s12[:, 0:1], scalar1=1.0 / CHUNK,
+                                    scalar2=0.0, op0=ALU.mult, op1=ALU.add)
+            sm = sml.tile([P, 1], F32, name="sm")
+            nc.gpsimd.tensor_tensor(out=sm[:], in0=s12[:, 0:1], in1=st[:, b, PACK - 1, s * 6 + 1:s * 6 + 2], op=ALU.mult)
+            nc.gpsimd.tensor_tensor(out=st[:, b, PACK - 1, s * 6 + 2:s * 6 + 3], in0=s12[:, 1:2], in1=sm[:],
+                                    op=ALU.subtract)
+
         def regroup(f):
             b, s = divmod(f, NCH)
             cols_f = slice(s * CHUNK, (s + 1) * CHUNK)
             grouped = grp.tile([P, CHUNK, PACK], BF16, name="grouped", align_bytes=64)
             nc.scalar.copy(out=grouped[:].rearrange("p (c i) j -> p c j i", i=4),
-                           in_=raw[b][:, :, cols_f].rearrange("p j (c i) -> p c j i", i=4))
+                           in_=raw[f][:].rearrange("p j (c i) -> p c j i", i=4))
             gr[f] = grouped
 
         def regroup_v(f):
+            grouped = grp.tile([P, CHUNK, PACK], BF16, name="grouped", align_bytes=64)
+            nc.vector.tensor_copy(out=grouped[:].rearrange("p (c i) j -> p c j i", i=4),
+                                  in_=raw[f][:].rearrange("p j (c i) -> p c j i", i=4))
+            gr[f] = grouped
+
+        def regroup_g(f):
             b, s = divmod(f, NCH)
             cols_f = slice(s * CHUNK, (s + 1) * CHUNK)
             grouped = grp.tile([P, CHUNK, PACK], BF16, name="grouped", align_bytes=64)
-            nc.vector.tensor_copy(out=grouped[:].rearrange("p (c i) j -> p c j i", i=4),
-                                  in_=raw[b][:, :, cols_f].rearrange("p j (c i) -> p c j i", i=4))
+            nc.gpsimd.tensor_scalar(out=grouped[:], in0=raw[f][:].rearrange("p j t -> p t j"),
+                                    scalar1=1.0, scalar2=0.0, op0=ALU.mult, op1=ALU.add)
             gr[f] = grouped
 
         def quant(f):
@@ -294,12 +392,13 @@ def tile_attentivestatspool_pa_t_kernel(tc, x, mask, w1, b1, g1, be1, out):
             ln[g] = (mu, sq)
 
         def var_v(g):
+            eng = nc.gpsimd if g in VEG else nc.vector
             ve = sml.tile([P, TILES], F32, name="ve")
             if g in VROUTE:
-                nc.vector.tensor_scalar(out=ve[:], in0=ln[g][:, :, 1], scalar1=1.0, scalar2=EPS_LN,
+                eng.tensor_scalar(out=ve[:], in0=ln[g][:, :, 1], scalar1=1.0, scalar2=EPS_LN,
                                         op0=ALU.mult, op1=ALU.add)
             else:
-                nc.vector.tensor_scalar(out=ve[:], in0=ln[g][1][:], scalar1=1.0 / H**3, scalar2=EPS_LN / H**2,
+                eng.tensor_scalar(out=ve[:], in0=ln[g][1][:], scalar1=1.0 / H**3, scalar2=EPS_LN / H**2,
                                         op0=ALU.mult, op1=ALU.add)
             ves[g] = ve
 
@@ -312,6 +411,10 @@ def tile_attentivestatspool_pa_t_kernel(tc, x, mask, w1, b1, g1, be1, out):
                 negmu = sml.tile([P, TILES], F32, name="negmu")
                 nc.gpsimd.tensor_scalar(out=negmu[:], in0=ln[g][0][:], scalar1=-1.0 / H, scalar2=0.0,
                                         op0=ALU.mult, op1=ALU.add)
+                if g in SNORM:
+                    nmr = sml.tile([P, TILES], F32, name="nmr")
+                    nc.gpsimd.tensor_tensor(out=nmr[:], in0=negmu[:], in1=rstd[:], op=ALU.mult)
+                    negmu = nmr
                 nrm[g] = [(negmu[:, k:k + 1], rstd[:, k:k + 1]) for k in range(TILES)]
 
         def relu_v(g):
@@ -330,6 +433,12 @@ def tile_attentivestatspool_pa_t_kernel(tc, x, mask, w1, b1, g1, be1, out):
         def normalise(g, eng):
             for k in range(TILES):
                 norm_piece(g, eng, k)
+
+        def normalise_s(g):
+            zhs[g] = zp.tile([P, TILES, H], F32, name="zh")
+            for k in range(TILES):
+                nmr, rstd = nrm[g][k]
+                nc.scalar.activation(out=zhs[g][:, k, :], in_=av[g][:, k, :], func=ACT.Identity, scale=rstd, bias=nmr)
 
         def norm_piece(g, eng, k):
             if k == 0:
@@ -366,13 +475,9 @@ def tile_attentivestatspool_pa_t_kernel(tc, x, mask, w1, b1, g1, be1, out):
 
         done = {"rg": 0, "q": 0}
 
-        def regroup_to(n):
-            while done["rg"] < min(NG, n):
-                if done["rg"] in VRG:
-                    regroup_v(done["rg"])
-                else:
-                    regroup(done["rg"])
-                done["rg"] = done["rg"] + 1
+        rg_s = {0: (4,), 1: (5,), 2: (6,), 3: (7,), 4: (8, 10), 5: (11,), 8: (12,), 9: (13,), 10: (14,), 11: (15,)}
+        rg_v = {}
+        rg_g = {6: (9,)}
 
         def quant_to(n):
             while done["q"] < min(NG, n):
@@ -381,67 +486,142 @@ def tile_attentivestatspool_pa_t_kernel(tc, x, mask, w1, b1, g1, be1, out):
 
         mask_bc(0)
         mask_mul(0)
-        for f in GMASK[0:2]:
+        for f in GM0:
             mask_bc(f)
-        regroup_to(1)
-        for f in GMASK[0:2]:
+        regroup(0)
+        regroup_g(1)
+        for f in GM0:
             mask_gp(f, nc.scalar.copy)
         columns()
         mask_bc(1)
-        regroup_to(RGA)
+        regroup(2)
+        regroup(3)
+        GB = set(f // NCH for f in GC)
+
+        def chain_close(b):
+            for j in range(PACK):
+                aggr(b, j)
+            std_of(b, nc.gpsimd)
+
         for f in range(NG):
             i = f - LEAD
             b, s = divmod(f, NCH)
+            late = b - 1 in GB
             if f == 4:
                 w1_quant()
-            if f >= 4:
-                quant_to(min(f, NG - NCH))
-            if s == 1 and b > 0:
+            if s == 1 and b > 0 and not late:
                 spread(b - 1)
                 spread_q(b - 1)
-            if f + 2 in GMASK[2:]:
-                mask_gp(f + 2, nc.vector.tensor_copy)
+            if f >= 4:
+                quant_to(min(f, NG - NCH))
+            for c in rg_g.get(f, ()):
+                regroup_g(c)
+            for c in rg_v.get(f, ()):
+                regroup_v(c)
             if ok(i - 2):
                 var_v(i - 2)
                 rstd_g(i - 2)
+            if s == 1 and b > 0 and late:
+                chain_close(b - 1)
             if f == 1:
                 ptot = totals_mm()
-            if ok(i - 3):
+            if s == 0 and late:
+                gram(b - 1, 0)
+                gram(b - 1, 1)
+            if ok(i - 3) and not (s == 0 and late):
                 p4(i - 3)
             if ok(i - 1):
                 relu_square(i - 1)
+            if f in SROW:
+                row_sums(f)
             if f == 1:
                 w1_transpose()
             if f == 2:
                 params()
             if f == 3:
                 params_b1()
-            if ok(i - 3):
+            if i - 2 in SNORM:
+                normalise_s(i - 2)
+            if ok(i - 3) and not (s == 0 and late):
                 tanh_store(i - 3)
-            regroup_to(f + 1 + RGA)
+            for c in rg_s.get(f, ()):
+                regroup(c)
+
+            def next_mask():
+                if f + 1 < NG and f + 1 not in GMASK and f + 1 not in GC:
+                    mask_mul(f + 1)
+                if f + 1 in GC:
+                    turn(f + 1, 0)
+                    turn(f + 1, 1)
+                elif f + 2 < NG and f + 2 not in GMASK and f + 2 not in GC:
+                    mask_bc(f + 2)
+
+            if f in GC:
+                turned_mask(f, 0)
+                if 0 <= i - 2 < NG - 2 * NCH and i - 2 not in SNORM:
+                    normalise(i - 2, nc.gpsimd)
+                if s == 1 and b > 0:
+                    bias_row(b - 1)
+                if ok(i):
+                    p1(i)
+                    mx(i + 1)
+                turned_mask(f, 1)
+                if f + 1 < NG and f + 1 not in GC and f + 1 not in GMASK:
+                    mask_bc(f + 1)
+                next_mask()
+                if i == -1:
+                    mx(0)
+                continue
             for j in range(PACK):
-                bn(f, j)
-                if j == 0 and s == 0 and b > 0:
+                if j < PACK - 1 or f not in SROW:
+                    bn(f, j)
+                if j == 2 and f in SROW:
+                    row_triple(f)
+                if j == 0 and s == 0 and b > 0 and not late:
                     aggr(b - 1, 3)
                     std_of(b - 1, nc.gpsimd)
-                if j == 0 and 0 <= i - 2 < NG - 2 * NCH:
+                if j == 0 and f == 4:
+                    for c in GMASK[len(GM0):]:
+                        mask_bc(c)
+                        mask_gp(c, nc.scalar.copy)
+                if j == 0 and 0 <= i - 2 < NG - 2 * NCH and i - 2 not in SNORM:
                     normalise(i - 2, nc.gpsimd)
-                if j > 0 and s == NCH - 1:
+                if j > 0 and s == NCH - 1 and b not in GB:
                     aggr(b, j - 1)
                 if j == 1:
-                    if f + 1 < NG and f + 1 not in GMASK:
-                        mask_mul(f + 1)
-                    if f + 2 < NG and f + 2 not in GMASK:
-                        mask_bc(f + 2)
-                    if f + 3 in GMASK[2:]:
-                        mask_bc(f + 3)
+                    next_mask()
+                if s == 0 and late:
+                    if j == 1:
+                        ext = gram_triple(b - 1, 0)
+                        ext[0]()
+                    if j == 2:
+                        ext[1]()
+                        if ok(i - 3):
+                            p4(i - 3)
+                            tanh_store(i - 3)
+                    if j == 3:
+                        ext[2]()
+                        ext = gram_triple(b - 1, 1)
+                        ext[0]()
                 if j == 2 and f == 1:
                     totals(ptot)
                 if j == 2 and s == 1 and b > 0:
+                    if late:
+                        spread(b - 1)
+                        spread_q(b - 1)
+                    else:
+                        bias_row(b - 1)
+                if j == 3 and s == 1 and b > 0 and late:
                     bias_row(b - 1)
             if i == -1:
                 mx(0)
-            if ok(i) and f < NG - 1:
+            if s == 0 and late:
+                p1_half(i, 0)
+                ext[1]()
+                p1_half(i, 1)
+                ext[2]()
+                mx(i + 1)
+            elif ok(i) and f < NG - 1:
                 p1(i)
                 mx(i + 1)
         b = B - 1
@@ -465,7 +645,6 @@ def tile_attentivestatspool_pa_t_kernel(tc, x, mask, w1, b1, g1, be1, out):
         relu_square(last - 1)
         tanh_store(last - 4)
         p1(last)
-        relu_square(last)
         quant_to(last + 3)
         mx(last + 1)
         normalise(last - 3, nc.vector)
@@ -476,34 +655,36 @@ def tile_attentivestatspool_pa_t_kernel(tc, x, mask, w1, b1, g1, be1, out):
         rstd_g(last - 1)
         p1(last + 1)
         mx(last + 2)
-        p1(last + 2)
-        quant_to(last + 4)
-        mx(last + 3)
         relu_square(last + 1)
         tanh_store(last - 3)
-        relu_v(last + 2)
+        relu_v(last)
+        stats_v(last)
+        p1(last + 2)
+        relu_square(last + 2)
         normalise(last - 2, nc.vector)
         p4(last - 2)
         tanh_store(last - 2)
+        var_v(last)
+        rstd_g(last)
+        quant_to(last + 4)
+        mx(last + 3)
         normalise(last - 1, nc.vector)
         p4(last - 1)
-        var_v(last)
-        var_v(last + 1)
-        rstd_g(last)
-        rstd_g(last + 1)
-        p1(last + 3)
-        relu_square(last + 3)
-        stats_v(last + 2)
         tanh_store(last - 1)
+        p1(last + 3)
+        var_v(last + 1)
+        rstd_g(last + 1)
+        relu_v(last + 3)
         normalise(last, nc.vector)
         p4(last)
         tanh_store(last)
+        stats_v(last + 3)
         normalise(last + 1, nc.vector)
         p4(last + 1)
         tanh_store(last + 1)
         var_v(last + 2)
-        var_v(last + 3)
         rstd_g(last + 2)
+        var_v(last + 3)
         rstd_g(last + 3)
         normalise(last + 2, nc.vector)
         p4(last + 2)

@@ -26,10 +26,14 @@ LEAD = 5
 RGA = 3
 RGB = 5
 SROW = []
-GM0 = [3, 4]
-GMASK = GM0 + [8]
-GC = [5, 6, 7]
-SNORM = [0]
+GSLOT = 15
+GM0 = [3]
+GM1 = [7, 8]
+GMASK = GM0 + GM1
+GC = [4, 5, 6]
+P3 = []
+SNORM = []
+NV = []
 VEG = list(range(0, 16))
 GRG = [1, 8, 9]
 VNORM_FROM = 10
@@ -111,8 +115,7 @@ def tile_attentivestatspool_pa_t_kernel(tc, x, mask, w1, b1, g1, be1, out):
             nc.vector.memset(xmt[f][:, :, :, P:P + 2], 1.0)
         for b in sorted(set(f // NCH for f in GC)):
             fs = [f for f in GC if f // NCH == b]
-            s = fs[0] % NCH
-            nc.vector.memset(st[:, b, :, s * 6:s * 6 + 1], float(len(fs) * CHUNK))
+            nc.vector.memset(st[:, b, :, GSLOT:GSLOT + 1], float(len(fs) * CHUNK))
         b1bc = const.tile([P, H], BF16, name="b1bc")
 
         def columns():
@@ -155,14 +158,15 @@ def tile_attentivestatspool_pa_t_kernel(tc, x, mask, w1, b1, g1, be1, out):
                                             identity=ident_f[:])
                 nc.scalar.copy(out=w1g[:, g].bitcast(F32), in_=pw[:].rearrange("q u h -> q h u"))
 
-        def w1_quant():
-            for g in range(3):
+        def w1_quant(gs):
+            for g in gs:
                 nc.vector.quantize_mx(out=w1c[:, g, :].bitcast(FP8X4), scales=w1s[:, g, :],
                                       in_=w1g[:, g].rearrange("q h j -> q (h j)"))
 
         xc = {}
         xs = {}
         vb = {}
+        rows = {}
         gr = {}
         mk = {}
         fin = {}
@@ -199,8 +203,9 @@ def tile_attentivestatspool_pa_t_kernel(tc, x, mask, w1, b1, g1, be1, out):
             mkb = xmg.tile([P, CHUNK], BF16, name="mkb")
             copy(out=mkb[:], in_=mk[f][:])
             xm = xmg.tile([P, PACK, CHUNK], BF16, name="xmg")
-            nc.gpsimd.tensor_tensor(out=xm[:], in0=raw[f][:],
-                                    in1=mkb[:].unsqueeze(1).to_broadcast([P, PACK, CHUNK]), op=ALU.mult)
+            for j in range(0, PACK, 1):
+                nc.gpsimd.tensor_tensor(out=xm[:, j:j + 1, :], in0=raw[f][:, j:j + 1, :],
+                                        in1=mkb[:].unsqueeze(1).to_broadcast([P, 1, CHUNK]), op=ALU.mult)
             xms[f] = xm
 
         def bn(f, j):
@@ -211,7 +216,8 @@ def tile_attentivestatspool_pa_t_kernel(tc, x, mask, w1, b1, g1, be1, out):
         gps = {}
 
         def turn(f, h):
-            xt = ps_tr.tile([P, 2, CHUNK], BF16, tag="tr", name="xt")
+            pool, tag = (ps_mk, "pmk") if h == 0 else (ps_tr, "tr")
+            xt = pool.tile([P, 2, CHUNK], BF16, tag=tag, name="xt")
             for n in range(2):
                 k = 2 * h + n
                 for j in range(PACK):
@@ -243,11 +249,11 @@ def tile_attentivestatspool_pa_t_kernel(tc, x, mask, w1, b1, g1, be1, out):
         def gram_triple(b, h):
             gp = gps[(b, h)]
             fs = [f for f in GC if f // NCH == b]
-            s = fs[0] % NCH
+            s = GSLOT
             n_f = len(fs) * CHUNK
             s2 = sml.tile([P, 2], F32, name="s2")
             sm = sml.tile([P, 2], F32, name="smg")
-            mean = st[:, b, 2 * h:2 * h + 2, s * 6 + 1]
+            mean = st[:, b, 2 * h:2 * h + 2, s + 1]
 
             def diagonals():
                 for n in range(2):
@@ -259,7 +265,7 @@ def tile_attentivestatspool_pa_t_kernel(tc, x, mask, w1, b1, g1, be1, out):
             return [
                 diagonals,
                 lambda: nc.vector.tensor_tensor(out=sm[:], in0=gp[:, :, P], in1=mean, op=ALU.mult),
-                lambda: nc.vector.tensor_tensor(out=st[:, b, 2 * h:2 * h + 2, s * 6 + 2], in0=s2[:], in1=sm[:],
+                lambda: nc.vector.tensor_tensor(out=st[:, b, 2 * h:2 * h + 2, s + 2], in0=s2[:], in1=sm[:],
                                                 op=ALU.subtract),
             ]
 
@@ -316,7 +322,8 @@ def tile_attentivestatspool_pa_t_kernel(tc, x, mask, w1, b1, g1, be1, out):
         def aggr(b, j):
             if j == 0:
                 fin[b] = {"mv": per.tile([P, PACK, 2], F32, name="mv")}
-            nc.vector.bn_aggr(out=fin[b]["mv"][:, j, :], in_=st[:, b, j, :])
+            first = GSLOT if any(f // NCH == b for f in GC) else 0
+            nc.vector.bn_aggr(out=fin[b]["mv"][:, j, :], in_=st[:, b, j, first:])
 
         def std_of(b, eng):
             mv = fin[b]["mv"]
@@ -336,6 +343,9 @@ def tile_attentivestatspool_pa_t_kernel(tc, x, mask, w1, b1, g1, be1, out):
             msc = per.tile([P, 2 * P], U8, name="msc", align_bytes=64)
             nc.vector.quantize_mx(out=mc[:].bitcast(FP8X4), scales=msc[:],
                                   in_=e["msb"][:].rearrange("p k w j -> p (k w j)"))
+            if b in P3:
+                rows[b] = (mc, msc)
+                return
             e["ps"] = ps_ms.tile([P, H], F32, tag="ms", name="ps_vb")
             for gi in range(2):
                 nc.tensor.matmul_mx(out=e["ps"][:], lhsT=mc[:, gi * P:(gi + 1) * P].bitcast(FP8X4),
@@ -362,10 +372,13 @@ def tile_attentivestatspool_pa_t_kernel(tc, x, mask, w1, b1, g1, be1, out):
                 ps = ps_mx.tile([P, 2, H], F32, name="ps")
                 for i in range(2):
                     t0 = s * CHUNK + (2 * pair + i) * P
-                    nc.tensor.matmul_mx(out=ps[:, i, :], lhsT=xc[b][:, t0:t0 + P].bitcast(FP8X4),
-                                        lhsT_scale=xs[b][:, t0:t0 + P],
-                                        rhs=w1c[:, 0, :].bitcast(FP8X4), rhs_scale=w1s[:, 0, :],
-                                        start=True, stop=True)
+                    stat = [(xc[b][:, t0:t0 + P], xs[b][:, t0:t0 + P])]
+                    if b in P3:
+                        stat += [(rows[b][0][:, n * P:(n + 1) * P], rows[b][1][:, n * P:(n + 1) * P]) for n in range(2)]
+                    for n in range(len(stat)):
+                        nc.tensor.matmul_mx(out=ps[:, i, :], lhsT=stat[n][0].bitcast(FP8X4), lhsT_scale=stat[n][1],
+                                            rhs=w1c[:, n, :].bitcast(FP8X4), rhs_scale=w1s[:, n, :],
+                                            start=(n == 0), stop=(n == len(stat) - 1))
                 pss[g].append(ps)
 
         def p1(g):
@@ -376,7 +389,7 @@ def tile_attentivestatspool_pa_t_kernel(tc, x, mask, w1, b1, g1, be1, out):
             if pair == 0:
                 av[g] = up.tile([P, TILES, H], F32, name="a")
             nc.vector.tensor_tensor(out=av[g][:, 2 * pair:2 * pair + 2, :], in0=pss[g][pair][:],
-                                    in1=vb[g // NCH][:].unsqueeze(1).to_broadcast([P, 2, H]), op=ALU.add)
+                                    in1=(b1bc if g // NCH in P3 else vb[g // NCH])[:].unsqueeze(1).to_broadcast([P, 2, H]), op=ALU.add)
 
         def relu_square(g):
             a = av[g]
@@ -473,16 +486,35 @@ def tile_attentivestatspool_pa_t_kernel(tc, x, mask, w1, b1, g1, be1, out):
         def ok(g):
             return 0 <= g < NG
 
-        done = {"rg": 0, "q": 0}
+        done = {"q": 0}
 
-        rg_s = {0: (4,), 1: (5,), 2: (6,), 3: (7,), 4: (8, 10), 5: (11,), 8: (12,), 9: (13,), 10: (14,), 11: (15,)}
+        rg_s = {0: (4,), 1: (5,), 2: (6,), 4: (8, 9), 5: (10, 11), 7: (12,), 8: (13,), 9: (14,), 10: (15,)}
+        rg_g = {3: (7,)}
         rg_v = {}
-        rg_g = {6: (9,)}
 
         def quant_to(n):
             while done["q"] < min(NG, n):
                 quant(done["q"])
                 done["q"] = done["q"] + 1
+
+        gram_at = {}
+        for f in GC:
+            gram_at[f // NCH] = f + 1
+        GB = [b for b in gram_at if gram_at[b] % NCH == NCH - 1]
+
+        def bias(b):
+            if b not in P3:
+                bias_row(b)
+
+        def spread_both(b):
+            spread(b)
+            spread_q(b)
+            if b in P3:
+                mx(NCH * b)
+
+        def mx_next(g):
+            if ok(g) and (g % NCH or g // NCH not in P3):
+                mx(g)
 
         mask_bc(0)
         mask_mul(0)
@@ -496,44 +528,43 @@ def tile_attentivestatspool_pa_t_kernel(tc, x, mask, w1, b1, g1, be1, out):
         mask_bc(1)
         regroup(2)
         regroup(3)
-        GB = set(f // NCH for f in GC)
-
-        def chain_close(b):
-            for j in range(PACK):
-                aggr(b, j)
-            std_of(b, nc.gpsimd)
-
         for f in range(NG):
             i = f - LEAD
             b, s = divmod(f, NCH)
-            late = b - 1 in GB
             if f == 4:
-                w1_quant()
-            if s == 1 and b > 0 and not late:
-                spread(b - 1)
-                spread_q(b - 1)
-            if f >= 4:
+                w1_quant([0])
+                aggr(0, 3)
+                std_of(0, nc.gpsimd)
+                w1_quant([1, 2])
+                quant_to(4)
+            if s == 0 and b - 1 in GB:
+                for j in range(PACK):
+                    aggr(b - 1, j)
+                std_of(b - 1, nc.gpsimd)
+            elif s == 0 and b > 1:
+                aggr(b - 1, 3)
+                std_of(b - 1, nc.gpsimd)
+            if s == 1 and b > 0:
+                spread_both(b - 1)
+            if f >= 5:
                 quant_to(min(f, NG - NCH))
             for c in rg_g.get(f, ()):
                 regroup_g(c)
-            for c in rg_v.get(f, ()):
-                regroup_v(c)
             if ok(i - 2):
                 var_v(i - 2)
                 rstd_g(i - 2)
-            if s == 1 and b > 0 and late:
-                chain_close(b - 1)
+                if i - 2 < NG - 2 * NCH and i - 2 not in SNORM and i - 2 not in NV:
+                    normalise(i - 2, nc.gpsimd)
             if f == 1:
                 ptot = totals_mm()
-            if s == 0 and late:
-                gram(b - 1, 0)
-                gram(b - 1, 1)
-            if ok(i - 3) and not (s == 0 and late):
+            if f == gram_at.get(b):
+                gram(b, 0)
+                gram(b, 1)
+            early = f not in GC and f != gram_at.get(b)
+            if ok(i - 3) and early:
                 p4(i - 3)
             if ok(i - 1):
                 relu_square(i - 1)
-            if f in SROW:
-                row_sums(f)
             if f == 1:
                 w1_transpose()
             if f == 2:
@@ -542,12 +573,16 @@ def tile_attentivestatspool_pa_t_kernel(tc, x, mask, w1, b1, g1, be1, out):
                 params_b1()
             if i - 2 in SNORM:
                 normalise_s(i - 2)
-            if ok(i - 3) and not (s == 0 and late):
+            if ok(i - 3) and early:
                 tanh_store(i - 3)
+            if f == 4:
+                for c in GM1:
+                    mask_bc(c)
+                    mask_gp(c, nc.scalar.copy)
             for c in rg_s.get(f, ()):
                 regroup(c)
 
-            def next_mask():
+            def next_front():
                 if f + 1 < NG and f + 1 not in GMASK and f + 1 not in GC:
                     mask_mul(f + 1)
                 if f + 1 in GC:
@@ -558,72 +593,63 @@ def tile_attentivestatspool_pa_t_kernel(tc, x, mask, w1, b1, g1, be1, out):
 
             if f in GC:
                 turned_mask(f, 0)
-                if 0 <= i - 2 < NG - 2 * NCH and i - 2 not in SNORM:
-                    normalise(i - 2, nc.gpsimd)
+                if f + 1 in GC:
+                    turn(f + 1, 0)
+                elif f + 1 < NG and f + 1 not in GMASK:
+                    mask_bc(f + 1)
                 if s == 1 and b > 0:
-                    bias_row(b - 1)
+                    turned_mask(f, 1)
+                    bias(b - 1)
                 if ok(i):
                     p1(i)
-                    mx(i + 1)
-                turned_mask(f, 1)
-                if f + 1 < NG and f + 1 not in GC and f + 1 not in GMASK:
-                    mask_bc(f + 1)
-                next_mask()
-                if i == -1:
-                    mx(0)
-                continue
-            for j in range(PACK):
-                if j < PACK - 1 or f not in SROW:
+                    mx_next(i + 1)
+                if not (s == 1 and b > 0):
+                    turned_mask(f, 1)
+                for c in rg_v.get(f, ()):
+                    regroup_v(c)
+                if f + 1 in GC:
+                    turn(f + 1, 1)
+                else:
+                    next_front()
+            else:
+                ext = None
+                for j in range(PACK):
                     bn(f, j)
-                if j == 2 and f in SROW:
-                    row_triple(f)
-                if j == 0 and s == 0 and b > 0 and not late:
-                    aggr(b - 1, 3)
-                    std_of(b - 1, nc.gpsimd)
-                if j == 0 and f == 4:
-                    for c in GMASK[len(GM0):]:
-                        mask_bc(c)
-                        mask_gp(c, nc.scalar.copy)
-                if j == 0 and 0 <= i - 2 < NG - 2 * NCH and i - 2 not in SNORM:
-                    normalise(i - 2, nc.gpsimd)
-                if j > 0 and s == NCH - 1 and b not in GB:
-                    aggr(b, j - 1)
-                if j == 1:
-                    next_mask()
-                if s == 0 and late:
+                    if j > 0 and s == NCH - 1 and b not in GB:
+                        aggr(b, j - 1)
                     if j == 1:
-                        ext = gram_triple(b - 1, 0)
-                        ext[0]()
-                    if j == 2:
-                        ext[1]()
-                        if ok(i - 3):
-                            p4(i - 3)
-                            tanh_store(i - 3)
-                    if j == 3:
-                        ext[2]()
-                        ext = gram_triple(b - 1, 1)
-                        ext[0]()
-                if j == 2 and f == 1:
-                    totals(ptot)
-                if j == 2 and s == 1 and b > 0:
-                    if late:
-                        spread(b - 1)
-                        spread_q(b - 1)
-                    else:
-                        bias_row(b - 1)
-                if j == 3 and s == 1 and b > 0 and late:
-                    bias_row(b - 1)
+                        next_front()
+                        for c in rg_v.get(f, ()):
+                            regroup_v(c)
+                    if f == gram_at.get(b):
+                        if j == 2:
+                            ext = gram_triple(b, 0)
+                            ext[0]()
+                        if j == 3:
+                            ext[1]()
+                            ext1 = gram_triple(b, 1)
+                            ext1[0]()
+                            ext[2]()
+                    if j == 2 and f == 1:
+                        totals(ptot)
+                    if j == 2 and s == 1 and b > 0:
+                        bias(b - 1)
+                if ext:
+                    p1_half(i, 0)
+                    ext1[1]()
+                    p1_half(i, 1)
+                    ext1[2]()
+                    mx_next(i + 1)
+                elif ok(i) and f < NG - 1:
+                    p1(i)
+                    mx_next(i + 1)
+            if ok(i - 3) and not early:
+                p4(i - 3)
+                tanh_store(i - 3)
+            if i - 2 in NV:
+                normalise(i - 2, nc.vector)
             if i == -1:
-                mx(0)
-            if s == 0 and late:
-                p1_half(i, 0)
-                ext[1]()
-                p1_half(i, 1)
-                ext[2]()
-                mx(i + 1)
-            elif ok(i) and f < NG - 1:
-                p1(i)
-                mx(i + 1)
+                mx_next(0)
         b = B - 1
         last = NG - NCH
         p1_half(last - 2, 0)
@@ -642,26 +668,26 @@ def tile_attentivestatspool_pa_t_kernel(tc, x, mask, w1, b1, g1, be1, out):
         bias_row(b)
         var_v(last - 3)
         rstd_g(last - 3)
+        normalise(last - 3, nc.gpsimd)
         relu_square(last - 1)
         tanh_store(last - 4)
         p1(last)
         quant_to(last + 3)
         mx(last + 1)
-        normalise(last - 3, nc.vector)
-        p4(last - 3)
         var_v(last - 2)
-        var_v(last - 1)
         rstd_g(last - 2)
+        normalise(last - 2, nc.gpsimd)
+        var_v(last - 1)
         rstd_g(last - 1)
         p1(last + 1)
         mx(last + 2)
+        p4(last - 3)
         relu_square(last + 1)
         tanh_store(last - 3)
         relu_v(last)
         stats_v(last)
         p1(last + 2)
         relu_square(last + 2)
-        normalise(last - 2, nc.vector)
         p4(last - 2)
         tanh_store(last - 2)
         var_v(last)

@@ -32,7 +32,7 @@ GM1 = [7, 8]
 GMASK = GM0 + GM1
 GC = [4, 5, 6]
 P3 = []
-SNORM = []
+SNORM = [4, 6]
 NV = []
 VEG = list(range(0, 16))
 GRG = [1, 8, 9]
@@ -538,6 +538,9 @@ def tile_attentivestatspool_pa_t_kernel(tc, x, mask, w1, b1, g1, be1, out):
                 w1_quant([1, 2])
                 quant_to(4)
             if s == 0 and b - 1 in GB:
+                left[0]()
+                quant_to(min(f, NG - NCH))
+                left[1]()
                 for j in range(PACK):
                     aggr(b - 1, j)
                 std_of(b - 1, nc.gpsimd)
@@ -622,23 +625,21 @@ def tile_attentivestatspool_pa_t_kernel(tc, x, mask, w1, b1, g1, be1, out):
                         for c in rg_v.get(f, ()):
                             regroup_v(c)
                     if f == gram_at.get(b):
-                        if j == 2:
-                            ext = gram_triple(b, 0)
-                            ext[0]()
                         if j == 3:
-                            ext[1]()
+                            ext = gram_triple(b, 0)
                             ext1 = gram_triple(b, 1)
-                            ext1[0]()
-                            ext[2]()
+                            ext[0]()
                     if j == 2 and f == 1:
                         totals(ptot)
                     if j == 2 and s == 1 and b > 0:
                         bias(b - 1)
                 if ext:
                     p1_half(i, 0)
-                    ext1[1]()
+                    ext[1]()
                     p1_half(i, 1)
-                    ext1[2]()
+                    ext[2]()
+                    ext1[0]()
+                    left = ext1[1:]
                     mx_next(i + 1)
                 elif ok(i) and f < NG - 1:
                     p1(i)
@@ -668,26 +669,26 @@ def tile_attentivestatspool_pa_t_kernel(tc, x, mask, w1, b1, g1, be1, out):
         bias_row(b)
         var_v(last - 3)
         rstd_g(last - 3)
-        normalise(last - 3, nc.gpsimd)
         relu_square(last - 1)
         tanh_store(last - 4)
         p1(last)
         quant_to(last + 3)
         mx(last + 1)
+        normalise(last - 3, nc.vector)
+        p4(last - 3)
         var_v(last - 2)
-        rstd_g(last - 2)
-        normalise(last - 2, nc.gpsimd)
         var_v(last - 1)
+        rstd_g(last - 2)
         rstd_g(last - 1)
         p1(last + 1)
         mx(last + 2)
-        p4(last - 3)
         relu_square(last + 1)
         tanh_store(last - 3)
         relu_v(last)
         stats_v(last)
         p1(last + 2)
         relu_square(last + 2)
+        normalise(last - 2, nc.vector)
         p4(last - 2)
         tanh_store(last - 2)
         var_v(last)

@@ -34,7 +34,7 @@ GC = [4, 5, 6]
 P3 = []
 SNORM = [4, 6]
 NV = []
-VEG = list(range(0, 16))
+VEG = [g for g in range(16) if g != 9]
 GRG = [1, 8, 9]
 VNORM_FROM = 10
 VROUTE = [12, 15]
@@ -491,6 +491,7 @@ def tile_attentivestatspool_pa_t_kernel(tc, x, mask, w1, b1, g1, be1, out):
         rg_s = {0: (4,), 1: (5,), 2: (6,), 4: (8, 9), 5: (10, 11), 7: (12,), 8: (13,), 9: (14,), 10: (15,)}
         rg_g = {3: (7,)}
         rg_v = {}
+        rg_w = {}
 
         def quant_to(n):
             while done["q"] < min(NG, n):
@@ -638,6 +639,8 @@ def tile_attentivestatspool_pa_t_kernel(tc, x, mask, w1, b1, g1, be1, out):
                     ext[1]()
                     p1_half(i, 1)
                     ext[2]()
+                    for c in rg_w.get(f, ()):
+                        regroup_v(c)
                     ext1[0]()
                     left = ext1[1:]
                     mx_next(i + 1)
@@ -686,9 +689,9 @@ def tile_attentivestatspool_pa_t_kernel(tc, x, mask, w1, b1, g1, be1, out):
         tanh_store(last - 3)
         relu_v(last)
         stats_v(last)
+        normalise(last - 2, nc.vector)
         p1(last + 2)
         relu_square(last + 2)
-        normalise(last - 2, nc.vector)
         p4(last - 2)
         tanh_store(last - 2)
         var_v(last)

@@ -28,11 +28,11 @@ RGB = 5
 SROW = []
 GSLOT = 15
 GM0 = [3]
-GM1 = [7, 8]
+GM1 = [7]
 GMASK = GM0 + GM1
 GC = [4, 5, 6]
 P3 = []
-SNORM = [4, 6]
+SNORM = [3, 5, 7]
 NV = []
 VEG = [g for g in range(16) if g != 9]
 GRG = [1, 8, 9]
@@ -488,8 +488,8 @@ def tile_attentivestatspool_pa_t_kernel(tc, x, mask, w1, b1, g1, be1, out):
 
         done = {"q": 0}
 
-        rg_s = {0: (4,), 1: (5,), 2: (6,), 4: (8, 9), 5: (10, 11), 7: (12,), 8: (13,), 9: (14,), 10: (15,)}
-        rg_g = {3: (7,)}
+        rg_s = {0: (4,), 1: (5,), 2: (6,), 4: (8,), 5: (11,), 6: (12,), 7: (13,), 8: (14,), 9: (15,)}
+        rg_g = {3: (7,), 5: (9,), 6: (10,)}
         rg_v = {}
         rg_w = {}
 

@@ -492,6 +492,7 @@ def tile_attentivestatspool_pa_t_kernel(tc, x, mask, w1, b1, g1, be1, out):
         rg_g = {3: (7,), 5: (9,), 6: (10,)}
         rg_v = {}
         rg_w = {}
+        rg_h = {}
 
         def quant_to(n):
             while done["q"] < min(NG, n):
@@ -507,8 +508,9 @@ def tile_attentivestatspool_pa_t_kernel(tc, x, mask, w1, b1, g1, be1, out):
             if b not in P3:
                 bias_row(b)
 
-        def spread_both(b):
+        def spread_both(b, n):
             spread(b)
+            quant_to(n)
             spread_q(b)
             if b in P3:
                 mx(NCH * b)
@@ -549,7 +551,7 @@ def tile_attentivestatspool_pa_t_kernel(tc, x, mask, w1, b1, g1, be1, out):
                 aggr(b - 1, 3)
                 std_of(b - 1, nc.gpsimd)
             if s == 1 and b > 0:
-                spread_both(b - 1)
+                spread_both(b - 1, min(f, NG - NCH))
             if f >= 5:
                 quant_to(min(f, NG - NCH))
             for c in rg_g.get(f, ()):
@@ -559,6 +561,8 @@ def tile_attentivestatspool_pa_t_kernel(tc, x, mask, w1, b1, g1, be1, out):
                 rstd_g(i - 2)
                 if i - 2 < NG - 2 * NCH and i - 2 not in SNORM and i - 2 not in NV:
                     normalise(i - 2, nc.gpsimd)
+            for c in rg_h.get(f, ()):
+                regroup_g(c)
             if f == 1:
                 ptot = totals_mm()
             if f == gram_at.get(b):
@@ -602,8 +606,8 @@ def tile_attentivestatspool_pa_t_kernel(tc, x, mask, w1, b1, g1, be1, out):
                 elif f + 1 < NG and f + 1 not in GMASK:
                     mask_bc(f + 1)
                 if s == 1 and b > 0:
-                    turned_mask(f, 1)
                     bias(b - 1)
+                    turned_mask(f, 1)
                 if ok(i):
                     p1(i)
                     mx_next(i + 1)
@@ -663,9 +667,7 @@ def tile_attentivestatspool_pa_t_kernel(tc, x, mask, w1, b1, g1, be1, out):
         mx(last - 1)
         relu_square(last - 2)
         p1(last - 1)
-        spread(b)
-        spread_q(b)
-        quant_to(last + 1)
+        spread_both(b, last + 1)
         mx(last)
         normalise(last - 4, nc.vector)
         p4(last - 4)

@@ -690,6 +690,7 @@ def tile_attentivestatspool_pa_t_kernel(tc, x, mask, w1, b1, g1, be1, out):
         relu_square(last + 1)
         tanh_store(last - 3)
         relu_v(last)
+        quant_to(last + 4)
         stats_v(last)
         normalise(last - 2, nc.vector)
         p1(last + 2)
@@ -698,7 +699,6 @@ def tile_attentivestatspool_pa_t_kernel(tc, x, mask, w1, b1, g1, be1, out):
         tanh_store(last - 2)
         var_v(last)
         rstd_g(last)
-        quant_to(last + 4)
         mx(last + 3)
         normalise(last - 1, nc.vector)
         p4(last - 1)

from contextlib import ExitStack

import concourse.mybir as mybir
from concourse.masks import make_identity

F32 = mybir.dt.float32
BF16 = mybir.dt.bfloat16
U32 = mybir.dt.uint32
U8 = mybir.dt.uint8
FP8X4 = mybir.dt.float8_e4m3fn_x4
ALU = mybir.AluOpType
ACT = mybir.ActivationFunctionType
AX = mybir.AxisListType

B, C, T, H = 4, 512, 2048, 256
P = 128
PACK = 4
CHUNK = 512
NCH = T // CHUNK
TILES = CHUNK // P
NG = B * NCH
NQ = T // P
EPS_LN = 1e-5
EPS_STD = 1e-5
LEAD = 5
RGA = 3
RGB = 5
SROW = []
GSLOT = 15
GM0 = [3]
GM1 = [7]
GMASK = GM0 + GM1
GC = [4, 5, 6]
P3 = []
SNORM = [3, 5, 7]
NV = []
VEG = [g for g in range(16) if g != 9]
GRG = [1, 8, 9]
VNORM_FROM = 10
VROUTE = [12, 15]
FLOPS = 2 * B * H * 3 * C * T


def tile_attentivestatspool_pa_t_kernel(tc, x, mask, w1, b1, g1, be1, out):
    nc = tc.nc
    with ExitStack() as ctx:
        const = ctx.enter_context(tc.tile_pool(name="const", bufs=1))
        rawp = ctx.enter_context(tc.tile_pool(name="rawp", bufs=10))
        xmp = ctx.enter_context(tc.tile_pool(name="xmp", bufs=2))
        xmg = ctx.enter_context(tc.tile_pool(name="xmg", bufs=3))
        grp = ctx.enter_context(tc.tile_pool(name="grp", bufs=8))
        cod = ctx.enter_context(tc.tile_pool(name="cod", bufs=3))
        sml = ctx.enter_context(tc.tile_pool(name="sml", bufs=6))
        per = ctx.enter_context(tc.tile_pool(name="per", bufs=2))
        up = ctx.enter_context(tc.tile_pool(name="up", bufs=5))
        zp = ctx.enter_context(tc.tile_pool(name="zp", bufs=3))
        op = ctx.enter_context(tc.tile_pool(name="op", bufs=4))
        ps_mx = ctx.enter_context(tc.psum_pool(name="ps_mx", bufs=3))
        ps_tr = ctx.enter_context(tc.psum_pool(name="ps_tr", bufs=3))
        ps_ms = ctx.enter_context(tc.psum_pool(name="ps_ms", bufs=1))
        ps_mk = ctx.enter_context(tc.psum_pool(name="ps_mk", bufs=1))
        ctx.enter_context(tc.manual_schedule())

        w1_sb = const.tile([P, 2, 3 * C], BF16, name="w1_sb")
        pr = const.tile([P, P], BF16, name="pr")
        prm = const.tile([P, P], BF16, name="prm")
        x_v = [x[b].rearrange("(p j) t -> p j t", j=PACK) for b in range(B)]
        raw = {}

        def load(f):
            b, s = divmod(f, NCH)
            raw[f] = rawp.tile([P, PACK, CHUNK], BF16, name="rawc")
            n = 2 if f == 0 else PACK
            for j in range(0, PACK, n):
                nc.sync.dma_start(out=raw[f][:, j:j + n, :], in_=x_v[b][:, j:j + n, s * CHUNK:(s + 1) * CHUNK])

        nc.scalar.dma_start(out=pr[0:B * NQ, :], in_=mask.rearrange("b o (q r) -> (b o q) r", r=P))
        nc.vector.memset(pr[B * NQ:P, :], 0.0)
        nc.vector.memset(prm[:], 0.0)
        for f in range(6):
            load(f)
        nc.sync.dma_start(out=w1_sb[:], in_=w1.rearrange("(hh p) k -> p hh k", p=P))
        nc.sync.dma_start(out=prm[0:2, :], in_=g1.rearrange("(r f) -> r f", f=P))
        nc.sync.dma_start(out=prm[2:4, :], in_=be1.rearrange("(r f) -> r f", f=P))
        nc.sync.dma_start(out=prm[4:6, :], in_=b1.rearrange("(r f) -> r f", f=P))
        for f in range(6, NG):
            load(f)

        ident_b = const.tile([P, P], BF16, name="ident_b")
        make_identity(nc, ident_b[:])
        ident_f = const.tile([P, P], F32, name="ident_f")
        make_identity(nc, ident_f[:])
        warm = const.tile([P, 1], F32, name="warm")
        nc.vector.memset(warm[:], 0.0)
        nc.scalar.activation(out=warm[:], in_=warm[:], func=ACT.Tanh)
        ones_t = const.tile([P, P], BF16, name="ones_t")
        nc.vector.memset(ones_t[:], 1.0)
        half = const.tile([P, PACK], F32, name="half")
        nc.vector.memset(half[:], 0.5)
        nhalf = const.tile([P, TILES], F32, name="nhalf")
        nc.vector.memset(nhalf[:], -0.5)

        w1c = const.tile([P, 3, H], U32, name="w1c", align_bytes=64)
        w1s = const.tile([P, 3, H], U8, name="w1s", align_bytes=64)
        w1g = const.tile([P, 3, H, PACK], BF16, name="w1g", align_bytes=64)
        cols = const.tile([P, B * NQ], BF16, name="cols")
        cols1 = const.tile([P, B * NQ], BF16, name="cols1")
        gb = const.tile([P, 4], F32, name="gb")
        b1c = const.tile([P, 2], BF16, name="b1c")
        st = const.tile([P, B, PACK, NCH * 6 + 3], F32, name="st")
        nc.vector.memset(st[:], 0.0)
        xmt = {}
        for f in GC:
            xmt[f] = const.tile([P, TILES, PACK, P + 2], BF16, name="xmt%d" % f)
            nc.vector.memset(xmt[f][:, :, :, P:P + 2], 1.0)
        for b in sorted(set(f // NCH for f in GC)):
            fs = [f for f in GC if f // NCH == b]
            nc.vector.memset(st[:, b, :, GSLOT:GSLOT + 1], float(len(fs) * CHUNK))
        b1bc = const.tile([P, H], BF16, name="b1bc")

        def columns():
            ps_pr = ps_ms.tile([P, P], BF16, tag="ms", name="ps_pr")
            nc.tensor.transpose(out=ps_pr[:], in_=pr[:], identity=ident_b[:])
            nc.vector.tensor_copy(out=cols[:], in_=ps_pr[:, 0:B * NQ])
            nc.vector.tensor_scalar(out=cols1[:], in0=ps_pr[:, 0:B * NQ], scalar1=-1.0, scalar2=None, op0=ALU.add)

        def totals_mm():
            ps_tot = ps_ms.tile([P, B * NQ], F32, tag="ms", name="ps_tot")
            nc.tensor.matmul(out=ps_tot[:], lhsT=ones_t[:], rhs=cols1[:], start=True, stop=True)
            return ps_tot

        def totals(ps_tot):
            nc.vector.tensor_reduce(out=st[:, :, :, NCH * 6], axis=AX.X, op=ALU.add,
                                    in_=ps_tot[:].rearrange("p (b q) -> p b q", b=B).unsqueeze(2)
                                    .to_broadcast([P, B, PACK, NQ]))

        def params():
            ps_par = ps_ms.tile([P, P], BF16, tag="ms", name="ps_par")
            nc.tensor.transpose(out=ps_par[:], in_=prm[:], identity=ident_b[:])
            nc.scalar.copy(out=gb[:], in_=ps_par[:, 0:4])
            nc.scalar.copy(out=b1c[:], in_=ps_par[:, 4:6])

        def params_b1():
            ps_b1 = ps_ms.tile([P, H], BF16, tag="ms", name="ps_b1")
            for hh in range(2):
                nc.tensor.transpose(out=ps_b1[:, hh * P:(hh + 1) * P],
                                    in_=b1c[:, hh:hh + 1].to_broadcast([P, P]), identity=ident_b[:])
            nc.scalar.copy(out=b1bc[:], in_=ps_b1[:])

        def w1_transpose():
            words = w1_sb[:].rearrange("p hh k -> p (hh k)").bitcast(F32)
            for g in range(3):
                pw = ps_tr.tile([P, 2, H], F32, tag="tr", name="pw")
                for u in range(2):
                    for hh in range(2):
                        w0 = hh * (3 * C // 2) + g * (C // 2)
                        nc.tensor.transpose(out=pw[:, u, hh * P:(hh + 1) * P], in_=words[:, w0 + u:w0 + C // 2:2],
                                            identity=ident_f[:])
                nc.scalar.copy(out=w1g[:, g].bitcast(F32), in_=pw[:].rearrange("q u h -> q h u"))

        def w1_quant(gs):
            for g in gs:
                nc.vector.quantize_mx(out=w1c[:, g, :].bitcast(FP8X4), scales=w1s[:, g, :],
                                      in_=w1g[:, g].rearrange("q h j -> q (h j)"))

        xc = {}
        xs = {}
        vb = {}
        rows = {}
        gr = {}
        mk = {}
        fin = {}

        def mask_bc(f):
            b, s = divmod(f, NCH)
            if f in GMASK:
                pmk = ps_tr.tile([P, CHUNK], BF16, tag="tr", name="pmk2")
            else:
                pmk = ps_mk.tile([P, CHUNK], BF16, name="pmk")
            for k in range(TILES):
                c = b * NQ + s * TILES + k
                if f == 0 or f in GM0:
                    nc.tensor.matmul(out=pmk[:, k * P:(k + 1) * P], lhsT=ident_b[:, c:c + 1].to_broadcast([P, P]),
                                     rhs=pr[:], start=True, stop=True)
                else:
                    nc.tensor.transpose(out=pmk[:, k * P:(k + 1) * P], in_=cols[:, c:c + 1].to_broadcast([P, P]),
                                        identity=ident_b[:])
            mk[f] = pmk

        xms = {}

        def mask_mul(f):
            b, s = divmod(f, NCH)
            xm = xmp.tile([P, PACK, CHUNK], BF16, name="xm")
            for j in range(0, PACK, 2 if f == 0 else PACK):
                n = 2 if f == 0 else PACK
                nc.vector.tensor_tensor(out=xm[:, j:j + n, :], in0=raw[f][:, j:j + n, :],
                                        in1=mk[f][:].unsqueeze(1).to_broadcast([P, n, CHUNK]), op=ALU.mult)
            xms[f] = xm

        def mask_gp(f, copy):
            b, s = divmod(f, NCH)
            mkb = xmg.tile([P, CHUNK], BF16, name="mkb")
            copy(out=mkb[:], in_=mk[f][:])
            xm = xmg.tile([P, PACK, CHUNK], BF16, name="xmg")
            for j in range(0, PACK, 1):
                nc.gpsimd.tensor_tensor(out=xm[:, j:j + 1, :], in0=raw[f][:, j:j + 1, :],
                                        in1=mkb[:].unsqueeze(1).to_broadcast([P, 1, CHUNK]), op=ALU.mult)
            xms[f] = xm

        def bn(f, j):
            b, s = divmod(f, NCH)
            nc.vector.bn_stats(out=st[:, b, j, s * 6:(s + 1) * 6], in_=xms[f][:, j, :])

        xts = {}
        gps = {}

        def turn(f, h):
            pool, tag = (ps_mk, "pmk") if h == 0 else (ps_tr, "tr")
            xt = pool.tile([P, 2, CHUNK], BF16, tag=tag, name="xt")
            for n in range(2):
                k = 2 * h + n
                for j in range(PACK):
                    nc.tensor.transpose(out=xt[:, n, j * P:(j + 1) * P], in_=raw[f][:, j, k * P:(k + 1) * P],
                                        identity=ident_b[:])
            xts[(f, h)] = xt

        def turned_mask(f, h):
            b, s = divmod(f, NCH)
            xt = xts.pop((f, h))
            for n in range(2):
                k = 2 * h + n
                c = b * NQ + s * TILES + k
                nc.vector.tensor_scalar(out=xmt[f][:, k, :, 0:P], in0=xt[:, n, :].rearrange("p (j q) -> p j q", j=PACK),
                                        scalar1=cols[:, c:c + 1], scalar2=None, op0=ALU.mult)

        def gram(b, h):
            pool, tag = (ps_ms, "ms") if h == 0 else (ps_tr, "tr")
            gp = pool.tile([P, 2, P + 1], F32, tag=tag, name="gp")
            fs = [f for f in GC if f // NCH == b]
            for n in range(2):
                j = 2 * h + n
                for f in fs:
                    for k in range(TILES):
                        nc.tensor.matmul(out=gp[:, n, :], lhsT=xmt[f][:, k, j, 0:P], rhs=xmt[f][:, k, j, 0:P + 1],
                                         start=(f == fs[0] and k == 0), stop=(f == fs[-1] and k == TILES - 1))
            gps[(b, h)] = gp

        def gram_triple(b, h):
            gp = gps[(b, h)]
            fs = [f for f in GC if f // NCH == b]
            s = GSLOT
            n_f = len(fs) * CHUNK
            s2 = sml.tile([P, 2], F32, name="s2")
            sm = sml.tile([P, 2], F32, name="smg")
            mean = st[:, b, 2 * h:2 * h + 2, s + 1]

            def diagonals():
                for n in range(2):
                    junk = zp.tile([P, P], F32, name="junkg")
                    nc.vector.scalar_tensor_tensor(out=junk[:], in0=gp[:, n, 0:P], scalar=1.0, in1=ident_f[:],
                                                   op0=ALU.mult, op1=ALU.mult, accum_out=s2[:, n:n + 1])
                nc.vector.tensor_scalar(out=mean, in0=gp[:, :, P], scalar1=1.0 / n_f, scalar2=None, op0=ALU.mult)

            return [
                diagonals,
                lambda: nc.vector.tensor_tensor(out=sm[:], in0=gp[:, :, P], in1=mean, op=ALU.mult),
                lambda: nc.vector.tensor_tensor(out=st[:, b, 2 * h:2 * h + 2, s + 2], in0=s2[:], in1=sm[:],
                                                op=ALU.subtract),
            ]

        srow = {}

        def row_sums(f):
            s12 = sml.tile([P, 2], F32, name="s12")
            for n, func in enumerate((ACT.Identity, ACT.Square)):
                junk = zp.tile([P, CHUNK], BF16, name="junkr")
                nc.scalar.activation(out=junk[:], in_=xms[f][:, PACK - 1, :], func=func, accum_out=s12[:, n:n + 1])
            srow[f] = s12

        def row_triple(f):
            b, s = divmod(f, NCH)
            s12 = srow[f]
            nc.gpsimd.tensor_scalar(out=st[:, b, PACK - 1, s * 6 + 1:s * 6 + 2], in0=s12[:, 0:1], scalar1=1.0 / CHUNK,
                                    scalar2=0.0, op0=ALU.mult, op1=ALU.add)
            sm = sml.tile([P, 1], F32, name="sm")
            nc.gpsimd.tensor_tensor(out=sm[:], in0=s12[:, 0:1], in1=st[:, b, PACK - 1, s * 6 + 1:s * 6 + 2], op=ALU.mult)
            nc.gpsimd.tensor_tensor(out=st[:, b, PACK - 1, s * 6 + 2:s * 6 + 3], in0=s12[:, 1:2], in1=sm[:],
                                    op=ALU.subtract)

        def regroup(f):
            b, s = divmod(f, NCH)
            cols_f = slice(s * CHUNK, (s + 1) * CHUNK)
            grouped = grp.tile([P, CHUNK, PACK], BF16, name="grouped", align_bytes=64)
            nc.scalar.copy(out=grouped[:].rearrange("p (c i) j -> p c j i", i=4),
                           in_=raw[f][:].rearrange("p j (c i) -> p c j i", i=4))
            gr[f] = grouped

        def regroup_v(f):
            grouped = grp.tile([P, CHUNK, PACK], BF16, name="grouped", align_bytes=64)
            nc.vector.tensor_copy(out=grouped[:].rearrange("p (c i) j -> p c j i", i=4),
                                  in_=raw[f][:].rearrange("p j (c i) -> p c j i", i=4))
            gr[f] = grouped

        def regroup_g(f):
            b, s = divmod(f, NCH)
            cols_f = slice(s * CHUNK, (s + 1) * CHUNK)
            grouped = grp.tile([P, CHUNK, PACK], BF16, name="grouped", align_bytes=64)
            nc.gpsimd.tensor_scalar(out=grouped[:], in0=raw[f][:].rearrange("p j t -> p t j"),
                                    scalar1=1.0, scalar2=0.0, op0=ALU.mult, op1=ALU.add)
            gr[f] = grouped

        def quant(f):
            b, s = divmod(f, NCH)
            cols_f = slice(s * CHUNK, (s + 1) * CHUNK)
            if s == 0:
                xc[b] = cod.tile([P, T], U32, name="xc", align_bytes=64)
                xs[b] = cod.tile([P, T], U8, name="xs", align_bytes=64)
            nc.vector.quantize_mx(out=xc[b][:, cols_f].bitcast(FP8X4), scales=xs[b][:, cols_f],
                                  in_=gr.pop(f)[:].rearrange("p w j -> p (w j)"))

        def aggr(b, j):
            if j == 0:
                fin[b] = {"mv": per.tile([P, PACK, 2], F32, name="mv")}
            first = GSLOT if any(f // NCH == b for f in GC) else 0
            nc.vector.bn_aggr(out=fin[b]["mv"][:, j, :], in_=st[:, b, j, first:])

        def std_of(b, eng):
            mv = fin[b]["mv"]
            v0 = per.tile([P, PACK], F32, name="v0")
            eng.tensor_scalar(out=v0[:], in0=mv[:, :, 1], scalar1=EPS_STD, scalar2=0.0, op0=ALU.max, op1=ALU.add)
            nc.gpsimd.tensor_tensor(out=mv[:, :, 1], in0=v0[:], in1=half[:], op=ALU.pow)

        def spread(b):
            e = fin[b]
            e["msb"] = per.tile([P, 2, P, PACK], BF16, name="msb", align_bytes=64)
            nc.vector.tensor_copy(out=e["msb"][:], in_=e["mv"][:].rearrange("p j k -> p k j").unsqueeze(2)
                                  .to_broadcast([P, 2, P, PACK]))

        def spread_q(b):
            e = fin[b]
            mc = per.tile([P, 2 * P], U32, name="mc", align_bytes=64)
            msc = per.tile([P, 2 * P], U8, name="msc", align_bytes=64)
            nc.vector.quantize_mx(out=mc[:].bitcast(FP8X4), scales=msc[:],
                                  in_=e["msb"][:].rearrange("p k w j -> p (k w j)"))
            if b in P3:
                rows[b] = (mc, msc)
                return
            e["ps"] = ps_ms.tile([P, H], F32, tag="ms", name="ps_vb")
            for gi in range(2):
                nc.tensor.matmul_mx(out=e["ps"][:], lhsT=mc[:, gi * P:(gi + 1) * P].bitcast(FP8X4),
                                    lhsT_scale=msc[:, gi * P:(gi + 1) * P],
                                    rhs=w1c[:, 1 + gi, :].bitcast(FP8X4), rhs_scale=w1s[:, 1 + gi, :],
                                    start=(gi == 0), stop=(gi == 1))

        def bias_row(b):
            vb[b] = per.tile([P, H], F32, name="vb")
            nc.vector.tensor_tensor(out=vb[b][:], in0=fin.pop(b)["ps"][:], in1=b1bc[:], op=ALU.add)

        pss = {}
        av = {}
        ln = {}
        nrm = {}
        ves = {}
        zhs = {}
        pts = {}

        def mx(g):
            b, s = divmod(g, NCH)
            pss[g] = []
            for pair in range(TILES // 2):
                ps = ps_mx.tile([P, 2, H], F32, name="ps")
                for i in range(2):
                    t0 = s * CHUNK + (2 * pair + i) * P
                    stat = [(xc[b][:, t0:t0 + P], xs[b][:, t0:t0 + P])]
                    if b in P3:
                        stat += [(rows[b][0][:, n * P:(n + 1) * P], rows[b][1][:, n * P:(n + 1) * P]) for n in range(2)]
                    for n in range(len(stat)):
                        nc.tensor.matmul_mx(out=ps[:, i, :], lhsT=stat[n][0].bitcast(FP8X4), lhsT_scale=stat[n][1],
                                            rhs=w1c[:, n, :].bitcast(FP8X4), rhs_scale=w1s[:, n, :],
                                            start=(n == 0), stop=(n == len(stat) - 1))
                pss[g].append(ps)

        def p1(g):
            for pair in range(TILES // 2):
                p1_half(g, pair)

        def p1_half(g, pair):
            if pair == 0:
                av[g] = up.tile([P, TILES, H], F32, name="a")
            nc.vector.tensor_tensor(out=av[g][:, 2 * pair:2 * pair + 2, :], in0=pss[g][pair][:],
                                    in1=(b1bc if g // NCH in P3 else vb[g // NCH])[:].unsqueeze(1).to_broadcast([P, 2, H]), op=ALU.add)

        def relu_square(g):
            a = av[g]
            mu = sml.tile([P, TILES], F32, name="mu")
            for k in range(TILES):
                nc.scalar.activation(out=a[:, k, :], in_=a[:, k, :], func=ACT.Relu, scale=1.0 / H,
                                     accum_out=mu[:, k:k + 1])
            sq = sml.tile([P, TILES], F32, name="sq")
            for k in range(TILES):
                junk = zp.tile([P, H], F32, name="junk")
                nc.scalar.activation(out=junk[:], in_=a[:, k, :], func=ACT.Square, scale=-float(H),
                                     bias=mu[:, k:k + 1], accum_out=sq[:, k:k + 1])
            ln[g] = (mu, sq)

        def var_v(g):
            eng = nc.gpsimd if g in VEG else nc.vector
            ve = sml.tile([P, TILES], F32, name="ve")
            if g in VROUTE:
                eng.tensor_scalar(out=ve[:], in0=ln[g][:, :, 1], scalar1=1.0, scalar2=EPS_LN,
                                        op0=ALU.mult, op1=ALU.add)
            else:
                eng.tensor_scalar(out=ve[:], in0=ln[g][1][:], scalar1=1.0 / H**3, scalar2=EPS_LN / H**2,
                                        op0=ALU.mult, op1=ALU.add)
            ves[g] = ve

        def rstd_g(g):
            rstd = sml.tile([P, TILES], F32, name="rstd")
            nc.gpsimd.tensor_tensor(out=rstd[:], in0=ves.pop(g)[:], in1=nhalf[:], op=ALU.pow)
            if g in VROUTE:
                nrm[g] = [(ln[g][:, k, 0:1], rstd[:, k:k + 1]) for k in range(TILES)]
            else:
                negmu = sml.tile([P, TILES], F32, name="negmu")
                nc.gpsimd.tensor_scalar(out=negmu[:], in0=ln[g][0][:], scalar1=-1.0 / H, scalar2=0.0,
                                        op0=ALU.mult, op1=ALU.add)
                if g in SNORM:
                    nmr = sml.tile([P, TILES], F32, name="nmr")
                    nc.gpsimd.tensor_tensor(out=nmr[:], in0=negmu[:], in1=rstd[:], op=ALU.mult)
                    negmu = nmr
                nrm[g] = [(negmu[:, k:k + 1], rstd[:, k:k + 1]) for k in range(TILES)]

        def relu_v(g):
            nc.vector.tensor_scalar(out=av[g][:], in0=av[g][:], scalar1=0.0, scalar2=None, op0=ALU.max)

        def stats_v(g):
            a = av[g]
            st4 = sml.tile([P, TILES, 6], F32, name="st4")
            mv4 = sml.tile([P, TILES, 2], F32, name="mv4")
            for k in range(TILES):
                nc.vector.bn_stats(out=st4[:, k, :], in_=a[:, k, :])
            for k in range(TILES):
                nc.vector.bn_aggr(out=mv4[:, k, :], in_=st4[:, k, :])
            ln[g] = mv4

        def normalise(g, eng):
            for k in range(TILES):
                norm_piece(g, eng, k)

        def normalise_s(g):
            zhs[g] = zp.tile([P, TILES, H], F32, name="zh")
            for k in range(TILES):
                nmr, rstd = nrm[g][k]
                nc.scalar.activation(out=zhs[g][:, k, :], in_=av[g][:, k, :], func=ACT.Identity, scale=rstd, bias=nmr)

        def norm_piece(g, eng, k):
            if k == 0:
                zhs[g] = zp.tile([P, TILES, H], F32, name="zh")
            mean, rstd = nrm[g][k]
            eng.tensor_scalar(out=zhs[g][:, k, :], in0=av[g][:, k, :], scalar1=mean, scalar2=rstd,
                              op0=ALU.subtract if g in VROUTE else ALU.add, op1=ALU.mult)

        def p4(g):
            zh = zhs.pop(g)
            pts[g] = []
            for hh in range(2):
                pt = ps_tr.tile([P, CHUNK], F32, tag="tr", name="pt")
                for k in range(TILES):
                    nc.tensor.transpose(out=pt[:, k * P:(k + 1) * P], in_=zh[:, k, hh * P:(hh + 1) * P],
                                        identity=ident_f[:])
                pts[g].append(pt)

        def tanh_store(g):
            b, s = divmod(g, NCH)
            o = op.tile([P, 2, CHUNK], F32, name="o")
            for hh in range(2):
                nc.scalar.activation(out=o[:, hh, :], in_=pts[g][hh][:], func=ACT.Tanh,
                                     scale=gb[:, hh:hh + 1], bias=gb[:, 2 + hh:3 + hh])
                if g == NG - 1:
                    nc.sync.dma_start(out=out[b][hh * P:(hh + 1) * P, s * CHUNK:(s + 1) * CHUNK], in_=o[:, hh, :])
            pts.pop(g)
            if g < NG - 1:
                nc.sync.dma_start(out=out[b].rearrange("(hh p) t -> p hh t", p=P)[:, :, s * CHUNK:(s + 1) * CHUNK],
                                  in_=o[:])

        def ok(g):
            return 0 <= g < NG

        done = {"q": 0}

        rg_s = {0: (4,), 1: (5,), 2: (6,), 4: (8,), 5: (11,), 6: (12,), 7: (13,), 8: (14,), 9: (15,)}
        rg_g = {3: (7,), 5: (9,), 6: (10,)}
        rg_v = {}
        rg_w = {}
        rg_h = {}

        def quant_to(n):
            while done["q"] < min(NG, n):
                quant(done["q"])
                done["q"] = done["q"] + 1

        gram_at = {}
        for f in GC:
            gram_at[f // NCH] = f + 1
        GB = [b for b in gram_at if gram_at[b] % NCH == NCH - 1]

        def bias(b):
            if b not in P3:
                bias_row(b)

        def spread_both(b, n):
            spread(b)
            quant_to(n)
            spread_q(b)
            if b in P3:
                mx(NCH * b)

        def mx_next(g):
            if ok(g) and (g % NCH or g // NCH not in P3):
                mx(g)

        mask_bc(0)
        mask_mul(0)
        for f in GM0:
            mask_bc(f)
        regroup(0)
        regroup_g(1)
        for f in GM0:
            mask_gp(f, nc.scalar.copy)
        columns()
        mask_bc(1)
        regroup(2)
        regroup(3)
        for f in range(NG):
            i = f - LEAD
            b, s = divmod(f, NCH)
            if f == 4:
                w1_quant([0])
                aggr(0, 3)
                std_of(0, nc.gpsimd)
                w1_quant([1, 2])
                quant_to(4)
            if s == 0 and b - 1 in GB:
                left[0]()
                quant_to(min(f, NG - NCH))
                left[1]()
                for j in range(PACK):
                    aggr(b - 1, j)
                std_of(b - 1, nc.gpsimd)
            elif s == 0 and b > 1:
                aggr(b - 1, 3)
                std_of(b - 1, nc.gpsimd)
            if s == 1 and b > 0:
                spread_both(b - 1, min(f, NG - NCH))
            if f >= 5:
                quant_to(min(f, NG - NCH))
            for c in rg_g.get(f, ()):
                regroup_g(c)
            if ok(i - 2):
                var_v(i - 2)
                rstd_g(i - 2)
                if i - 2 < NG - 2 * NCH and i - 2 not in SNORM and i - 2 not in NV:
                    normalise(i - 2, nc.gpsimd)
            for c in rg_h.get(f, ()):
                regroup_g(c)
            if f == 1:
                ptot = totals_mm()
            if f == gram_at.get(b):
                gram(b, 0)
                gram(b, 1)
            early = f not in GC and f != gram_at.get(b)
            if ok(i - 3) and early:
                p4(i - 3)
            if ok(i - 1):
                relu_square(i - 1)
            if f == 1:
                w1_transpose()
            if f == 2:
                params()
            if f == 3:
                params_b1()
            if i - 2 in SNORM:
                normalise_s(i - 2)
            if ok(i - 3) and early:
                tanh_store(i - 3)
            if f == 4:
                for c in GM1:
                    mask_bc(c)
                    mask_gp(c, nc.scalar.copy)
            for c in rg_s.get(f, ()):
                regroup(c)

            def next_front():
                if f + 1 < NG and f + 1 not in GMASK and f + 1 not in GC:
                    mask_mul(f + 1)
                if f + 1 in GC:
                    turn(f + 1, 0)
                    turn(f + 1, 1)
                elif f + 2 < NG and f + 2 not in GMASK and f + 2 not in GC:
                    mask_bc(f + 2)

            if f in GC:
                turned_mask(f, 0)
                if f + 1 in GC:
                    turn(f + 1, 0)
                elif f + 1 < NG and f + 1 not in GMASK:
                    mask_bc(f + 1)
                if s == 1 and b > 0:
                    bias(b - 1)
                    turned_mask(f, 1)
                if ok(i):
                    p1(i)
                    mx_next(i + 1)
                if not (s == 1 and b > 0):
                    turned_mask(f, 1)
                for c in rg_v.get(f, ()):
                    regroup_v(c)
                if f + 1 in GC:
                    turn(f + 1, 1)
                else:
                    next_front()
            else:
                ext = None
                for j in range(PACK):
                    bn(f, j)
                    if j > 0 and s == NCH - 1 and b not in GB:
                        aggr(b, j - 1)
                    if j == 1:
                        next_front()
                        for c in rg_v.get(f, ()):
                            regroup_v(c)
                    if f == gram_at.get(b):
                        if j == 3:
                            ext = gram_triple(b, 0)
                            ext1 = gram_triple(b, 1)
                            ext[0]()
                    if j == 2 and f == 1:
                        totals(ptot)
                    if j == 2 and s == 1 and b > 0:
                        bias(b - 1)
                if ext:
                    p1_half(i, 0)
                    ext[1]()
                    p1_half(i, 1)
                    ext[2]()
                    for c in rg_w.get(f, ()):
                        regroup_v(c)
                    ext1[0]()
                    left = ext1[1:]
                    mx_next(i + 1)
                elif ok(i) and f < NG - 1:
                    p1(i)
                    mx_next(i + 1)
            if ok(i - 3) and not early:
                p4(i - 3)
                tanh_store(i - 3)
            if i - 2 in NV:
                normalise(i - 2, nc.vector)
            if i == -1:
                mx_next(0)
        b = B - 1
        last = NG - NCH
        p1_half(last - 2, 0)
        aggr(b, 3)
        std_of(b, nc.vector)
        p1_half(last - 2, 1)
        mx(last - 1)
        relu_square(last - 2)
        p1(last - 1)
        spread_both(b, last + 1)
        mx(last)
        normalise(last - 4, nc.vector)
        p4(last - 4)
        bias_row(b)
        var_v(last - 3)
        rstd_g(last - 3)
        relu_square(last - 1)
        tanh_store(last - 4)
        p1(last)
        quant_to(last + 3)
        mx(last + 1)
        normalise(last - 3, nc.vector)
        p4(last - 3)
        var_v(last - 2)
        var_v(last - 1)
        rstd_g(last - 2)
        rstd_g(last - 1)
        p1(last + 1)
        mx(last + 2)
        relu_square(last + 1)
        tanh_store(last - 3)
        relu_v(last)
        quant_to(last + 4)
        stats_v(last)
        normalise(last - 2, nc.vector)
        p1(last + 2)
        relu_square(last + 2)
        p4(last - 2)
        tanh_store(last - 2)
        var_v(last)
        rstd_g(last)
        mx(last + 3)
        normalise(last - 1, nc.vector)
        p4(last - 1)
        tanh_store(last - 1)
        p1(last + 3)
        var_v(last + 1)
        rstd_g(last + 1)
        relu_v(last + 3)
        normalise(last, nc.vector)
        p4(last)
        tanh_store(last)
        stats_v(last + 3)
        normalise(last + 1, nc.vector)
        p4(last + 1)
        tanh_store(last + 1)
        var_v(last + 2)
        rstd_g(last + 2)
        var_v(last + 3)
        rstd_g(last + 3)
        normalise(last + 2, nc.vector)
        p4(last + 2)
        tanh_store(last + 2)
        normalise(last + 3, nc.vector)
        p4(last + 3)
        tanh_store(last + 3)
